import numpy as np
import ml_dtypes

BF16 = ml_dtypes.bfloat16


def bf(x):
    return np.asarray(x, np.float32).astype(BF16)


def f32(x):
    return np.asarray(x, np.float32)


def f64(x):
    return np.asarray(x).astype(np.float64)


def striped(idx):
    return np.tile(idx.reshape(-1, 16).T, (8, 1))


V, D, T, O, H, K, N = 1024, 128, 2048, 512, 512, 8, 4096
L1 = 0.5


def causal_softmax(a):
    keep = np.tril(np.ones(a.shape, bool))
    a = np.where(keep, a, -np.inf)
    p = np.exp(a - a.max(axis=1, keepdims=True))
    return p / p.sum(axis=1, keepdims=True)


def setup_inputs():
    return {
        "table": bf(np.random.standard_normal((V, D))),
        "w_right": bf(np.random.standard_normal((D, D)) / np.sqrt(D)),
        "w_wrong": bf(np.random.standard_normal((D, D)) / np.sqrt(D)),
        "b_in": f32(0.1 * np.random.standard_normal((D, 1))),
        "lab": f32(np.random.random((1, T)) < 0.5),
        "wq": bf(2.0 * np.random.standard_normal((D, D)) / np.sqrt(D)),
        "bq": f32(0.5 * np.random.standard_normal((D, 1))),
        "wk": bf(2.0 * np.random.standard_normal((D, D)) / np.sqrt(D)),
        "wv": bf(2.0 * np.random.standard_normal((D, D)) / np.sqrt(D)),
        "bv": f32(0.1 * np.random.standard_normal((D, 1))),
        "rel": f32(2.0 * np.random.standard_normal((T, T))),
        "w_out": bf(np.random.standard_normal((D, O)) / np.sqrt(D)),
        "b_out": f32(0.1 * np.random.standard_normal((O, 1))),
        "offs": striped(np.concatenate([np.random.permutation(V)[:H] for _ in range(K)])),
    }


def reference(table, w_right, w_wrong, b_in, lab, wq, bq, wk, wv, bv, rel, w_out, b_out, offs):
    idx = offs[:16].T.reshape(-1)
    e = f64(table)[idx].T
    eh, eq = e[:, :T], e[:, T:N]
    lb = f64(lab)
    x = np.maximum(lb * (f64(w_right).T @ eh) + (1.0 - lb) * (f64(w_wrong).T @ eh) + f64(b_in), 0.0)
    qm = f64(wq).T @ eq + f64(bq)
    km = f64(wk).T @ x
    vm = f64(wv).T @ x + f64(bv)
    sc = (qm.T @ km) / np.sqrt(D)
    attn = (1.0 - L1) * causal_softmax(sc) + L1 * causal_softmax(f64(rel))
    o = vm @ attn.T
    return f64(w_out).T @ o + f64(b_out)

@@ -1,0 +1,192 @@
+from contextlib import ExitStack
+
+import concourse.mybir as mybir
+from concourse.masks import make_identity
+
+BF16, F32, U16 = mybir.dt.bfloat16, mybir.dt.float32, mybir.dt.uint16
+ALU = mybir.AluOpType
+FUNC = mybir.ActivationFunctionType
+
+P = 128
+ITEMS = 1024
+T = 2048
+OUT = 512
+PIECE = 512
+BLOCKS = T // P
+PER_BANK = PIECE // P
+SCALE = 1.0 / 128.0**0.5
+MASKED = -1.0e30
+
+PAIRS = T * (T + 1) // 2
+FLOPS = 2 * P * (3 * P * T + 2 * P * T + 2 * PAIRS + OUT * T)
+BYTES = 4 * PAIRS + 4 * OUT * T + 2 * ITEMS * P + 2 * P * (5 * P + OUT) + 2 * 2 * T + 4 * T
+
+
+def tile_rkt_b_kernel(
+    tc, table, w_right, w_wrong, b_in, lab, wq, bq, wk, wv, bv, rel, w_out, b_out, offs, out
+):
+    nc = tc.nc
+    with ExitStack() as ctx:
+        held = ctx.enter_context(tc.tile_pool(name="held", bufs=1))
+        rel_pool = ctx.enter_context(tc.tile_pool(name="rel_pool", bufs=4))
+        rel_exp_pool = ctx.enter_context(tc.tile_pool(name="rel_exp_pool", bufs=8))
+        work = ctx.enter_context(tc.tile_pool(name="work", bufs=2))
+        stats = ctx.enter_context(tc.tile_pool(name="stats", bufs=4))
+        store = ctx.enter_context(tc.tile_pool(name="store", bufs=4))
+        product = ctx.enter_context(tc.psum_pool(name="product", bufs=4))
+        flip = ctx.enter_context(tc.psum_pool(name="flip", bufs=2))
+        mixed = ctx.enter_context(tc.psum_pool(name="mixed", bufs=2))
+
+        offsets = held.tile([P, 2 * T // 16], U16, name="offsets")
+        nc.sync.dma_start(offsets[:], offs)
+        table_rows = held.tile([P, ITEMS // P, P], BF16, name="table_rows")
+        nc.sync.dma_start(table_rows[:], table.rearrange("(a p) d -> p a d", p=P))
+
+        weights = {}
+        for name, w in (("right", w_right), ("wrong", w_wrong), ("q", wq), ("k", wk), ("v", wv), ("out", w_out)):
+            weights[name] = held.tile([P, w.shape[1]], BF16, name="w_" + name)
+            nc.scalar.dma_start(weights[name][:], w)
+
+        b_in_col = held.tile([P, 1], F32, name="b_in_col")
+        nc.gpsimd.dma_start(b_in_col[:], b_in)
+        bq_col = held.tile([P, 1], F32, name="bq_col")
+        nc.gpsimd.dma_start(bq_col[:], bq)
+        b_out_cols = held.tile([P, OUT // P], F32, name="b_out_cols")
+        with nc.allow_non_contiguous_dma(reason="one float32 to a partition and block"):
+            nc.gpsimd.dma_start(b_out_cols[:], b_out.rearrange("(a p) o -> p (a o)", p=P))
+        right_mask = held.tile([P, T], F32, name="right_mask")
+        nc.gpsimd.dma_start(right_mask[:], lab.rearrange("o t -> (o t)").partition_broadcast(P))
+        bv_rows = held.tile([P, P], F32, name="bv_rows")
+        nc.gpsimd.dma_start(bv_rows[:], bv.rearrange("e o -> (e o)").partition_broadcast(P))
+        wrong_mask = held.tile([P, T], F32, name="wrong_mask")
+        nc.gpsimd.tensor_scalar(wrong_mask[:], right_mask[:], -1.0, 1.0, ALU.mult, ALU.add)
+
+        identity = held.tile([P, P], BF16, name="identity")
+        make_identity(nc, identity[:])
+        future = held.tile([P, P], BF16, name="future")
+        nc.gpsimd.memset(future[:], 0.0)
+        nc.gpsimd.affine_select(
+            out=future[:], in_=future[:], pattern=[[-1, P]], compare_op=ALU.is_ge,
+            fill=MASKED, base=0, channel_multiplier=1,
+        )
+
+        flipped = flip.tile([P, ITEMS], BF16, name="flipped", tag="flip")
+        for a in range(ITEMS // P):
+            nc.tensor.transpose(flipped[:, a * P : (a + 1) * P], table_rows[:, a, :], identity[:])
+        window = held.tile([P, ITEMS], BF16, name="window")
+        nc.vector.tensor_copy(window[:], flipped[:])
+
+        def looked_up(piece):
+            return window[:].indirect(offsets[:, piece * (PIECE // 16) : (piece + 1) * (PIECE // 16)])
+
+        q_sb = held.tile([P, T], BF16, name="q_sb")
+        for piece in range(T // PIECE):
+            cols = slice(piece * PIECE, (piece + 1) * PIECE)
+            q_ps = product.tile([P, PIECE], F32, name="q_ps", tag="product")
+            nc.tensor.matmul(q_ps[:], weights["q"][:], looked_up(T // PIECE + piece), start=True, stop=True)
+            nc.scalar.activation(q_sb[:, cols], q_ps[:], FUNC.Identity, bias=bq_col[:, 0:1])
+
+        x_right = held.tile([P, T], BF16, name="x_right")
+        x_wrong = held.tile([P, T], BF16, name="x_wrong")
+        for piece in range(T // PIECE):
+            cols = slice(piece * PIECE, (piece + 1) * PIECE)
+            for w_name, mask, masked in (("right", right_mask, x_right), ("wrong", wrong_mask, x_wrong)):
+                x_ps = product.tile([P, PIECE], F32, name="x_ps", tag="product")
+                nc.tensor.matmul(x_ps[:], weights[w_name][:], looked_up(piece), start=True, stop=True)
+                nc.vector.scalar_tensor_tensor(
+                    out=masked[:, cols], in0=x_ps[:], scalar=b_in_col[:, 0:1], in1=mask[:, cols],
+                    op0=ALU.add, op1=ALU.mult,
+                )
+        x_sb = held.tile([P, T], BF16, name="x_sb")
+        nc.vector.tensor_tensor(x_sb[:], x_right[:], x_wrong[:], ALU.max)
+
+        k_sb = held.tile([P, T], BF16, name="k_sb")
+        for piece in range(T // PIECE):
+            cols = slice(piece * PIECE, (piece + 1) * PIECE)
+            k_ps = product.tile([P, PIECE], F32, name="k_ps", tag="product")
+            nc.tensor.matmul(k_ps[:], weights["k"][:], x_sb[:, cols], start=True, stop=True)
+            nc.vector.tensor_copy(k_sb[:, cols], k_ps[:])
+        v_sb = held.tile([P, BLOCKS, P], BF16, name="v_sb")
+        for first in range(0, BLOCKS, PER_BANK):
+            v_ps = product.tile([P, PER_BANK, P], F32, name="v_ps", tag="product")
+            for b in range(PER_BANK):
+                j = first + b
+                nc.tensor.matmul(v_ps[:, b, :], x_sb[:, j * P : (j + 1) * P], weights["v"][:], start=True, stop=True)
+            nc.vector.tensor_tensor(
+                v_sb[:, first : first + PER_BANK, :], v_ps[:],
+                bv_rows[:].unsqueeze(1).to_broadcast([P, PER_BANK, P]), ALU.add,
+            )
+
+        o_sb = held.tile([P, T], BF16, name="o_sb")
+        for i in reversed(range(BLOCKS)):
+            width = (i + 1) * P
+            queries = slice(i * P, width)
+            sums = stats.tile([P, 2], F32, name="sums")
+
+            rel_sb = rel_pool.tile([P, T], F32, name="rel_sb")
+            nc.sync.dma_start(rel_sb[:, :width], rel[queries, :width])
+            nc.gpsimd.affine_select(
+                out=rel_sb[:, queries], in_=rel_sb[:, queries], pattern=[[-1, P]], compare_op=ALU.is_ge,
+                fill=MASKED, base=0, channel_multiplier=1,
+            )
+            rel_shift = stats.tile([P, 1], F32, name="rel_shift")
+            nc.vector.tensor_reduce(
+                out=rel_shift[:], in_=rel_sb[:, :width], axis=mybir.AxisListType.X, op=ALU.max, negate=True
+            )
+            rel_exp = rel_exp_pool.tile([P, T], BF16, name="rel_exp")
+            nc.scalar.activation(
+                rel_exp[:, :width], rel_sb[:, :width], FUNC.Exp, bias=rel_shift[:, 0:1], accum_out=sums[:, 1:2]
+            )
+
+            minus_sc = work.tile([P, T], F32, name="minus_sc")
+            sc_shift = stats.tile([P, PER_BANK], F32, name="sc_shift")
+            banks = (width + PIECE - 1) // PIECE
+            for c in range(banks):
+                w = min(PIECE, width - c * PIECE)
+                sc_ps = product.tile([P, PIECE], F32, name="sc_ps", tag="product")
+                last = c == banks - 1
+                nc.tensor.matmul(
+                    sc_ps[:, :w], q_sb[:, queries], k_sb[:, c * PIECE : c * PIECE + w], start=True, stop=not last
+                )
+                if last:
+                    nc.tensor.matmul(sc_ps[:, w - P : w], identity[:], future[:], start=False, stop=True)
+                nc.vector.tensor_scalar(
+                    out=minus_sc[:, c * PIECE : c * PIECE + w], in0=sc_ps[:, :w], scalar1=-SCALE,
+                    scalar2=None if c == 0 else sc_shift[:, c - 1 : c], op0=ALU.mult, op1=ALU.min,
+                    accum_out=sc_shift[:, c : c + 1],
+                )
+            sc_exp = work.tile([P, T], BF16, name="sc_exp")
+            nc.scalar.activation(
+                sc_exp[:, :width], minus_sc[:, :width], FUNC.Exp, bias=sc_shift[:, banks - 1 : banks], scale=-1.0,
+                accum_out=sums[:, 0:1],
+            )
+
+            inverse = stats.tile([P, 2], F32, name="inverse")
+            nc.vector.reciprocal(inverse[:], sums[:])
+            sc_diag = work.tile([P, P], BF16, name="sc_diag")
+            nc.vector.tensor_scalar(sc_diag[:], identity[:], inverse[:, 0:1], None, ALU.mult)
+            rel_diag = work.tile([P, P], BF16, name="rel_diag")
+            nc.vector.tensor_scalar(rel_diag[:], identity[:], inverse[:, 1:2], None, ALU.mult)
+            a_sb = work.tile([P, BLOCKS, P], BF16, name="a_sb")
+            for first in range(0, i + 1, PER_BANK):
+                count = min(PER_BANK, i + 1 - first)
+                a_ps = flip.tile([P, PER_BANK, P], F32, name="a_ps", tag="flip")
+                for b in range(count):
+                    history = slice((first + b) * P, (first + b + 1) * P)
+                    nc.tensor.matmul(a_ps[:, b, :], sc_exp[:, history], sc_diag[:], start=True, stop=False)
+                    nc.tensor.matmul(a_ps[:, b, :], rel_exp[:, history], rel_diag[:], start=False, stop=True)
+                nc.vector.tensor_copy(a_sb[:, first : first + count, :], a_ps[:, :count, :])
+
+            o_ps = mixed.tile([P, P], F32, name="o_ps")
+            for j in range(i + 1):
+                nc.tensor.matmul(o_ps[:], v_sb[:, j, :], a_sb[:, j, :], start=j == 0, stop=j == i)
+            nc.scalar.mul(o_sb[:, queries], o_ps[:], 0.5)
+
+            if i % PER_BANK == 0:
+                cols = slice(i * P, i * P + PIECE)
+                for m in range(OUT // P):
+                    out_ps = product.tile([P, PIECE], F32, name="out_ps", tag="product")
+                    nc.tensor.matmul(out_ps[:], weights["out"][:, m * P : (m + 1) * P], o_sb[:, cols], start=True, stop=True)
+                    out_sb = store.tile([P, PIECE], F32, name="out_sb")
+                    nc.scalar.activation(out_sb[:], out_ps[:], FUNC.Identity, bias=b_out_cols[:, m : m + 1])
+                    nc.gpsimd.dma_start(out[m * P : (m + 1) * P, cols], out_sb[:])

@@ -14,6 +14,9 @@ OUT = 512
 PIECE = 512
 BLOCKS = T // P
 PER_BANK = PIECE // P
+PER_FLIP = 2 * PER_BANK
+LOADS_AHEAD = 4
+REL_AHEAD = 2
 SCALE = 1.0 / 128.0**0.5
 MASKED = -1.0e30
 
@@ -28,165 +31,233 @@ def tile_rkt_b_kernel(
     nc = tc.nc
     with ExitStack() as ctx:
         held = ctx.enter_context(tc.tile_pool(name="held", bufs=1))
-        rel_pool = ctx.enter_context(tc.tile_pool(name="rel_pool", bufs=4))
-        rel_exp_pool = ctx.enter_context(tc.tile_pool(name="rel_exp_pool", bufs=8))
-        work = ctx.enter_context(tc.tile_pool(name="work", bufs=2))
-        stats = ctx.enter_context(tc.tile_pool(name="stats", bufs=4))
+        rel_pool = ctx.enter_context(tc.tile_pool(name="rel_pool", bufs=LOADS_AHEAD))
+        rel_done = ctx.enter_context(tc.tile_pool(name="rel_done", bufs=REL_AHEAD + 3))
+        work = ctx.enter_context(tc.tile_pool(name="work", bufs=3))
         store = ctx.enter_context(tc.tile_pool(name="store", bufs=4))
         product = ctx.enter_context(tc.psum_pool(name="product", bufs=4))
         flip = ctx.enter_context(tc.psum_pool(name="flip", bufs=2))
         mixed = ctx.enter_context(tc.psum_pool(name="mixed", bufs=2))
 
         offsets = held.tile([P, 2 * T // 16], U16, name="offsets")
-        nc.sync.dma_start(offsets[:], offs)
         table_rows = held.tile([P, ITEMS // P, P], BF16, name="table_rows")
-        nc.sync.dma_start(table_rows[:], table.rearrange("(a p) d -> p a d", p=P))
-
+        window = held.tile([P, ITEMS], BF16, name="window")
         weights = {}
         for name, w in (("right", w_right), ("wrong", w_wrong), ("q", wq), ("k", wk), ("v", wv), ("out", w_out)):
             weights[name] = held.tile([P, w.shape[1]], BF16, name="w_" + name)
-            nc.scalar.dma_start(weights[name][:], w)
-
         b_in_col = held.tile([P, 1], F32, name="b_in_col")
-        nc.gpsimd.dma_start(b_in_col[:], b_in)
         bq_col = held.tile([P, 1], F32, name="bq_col")
-        nc.gpsimd.dma_start(bq_col[:], bq)
         b_out_cols = held.tile([P, OUT // P], F32, name="b_out_cols")
-        with nc.allow_non_contiguous_dma(reason="one float32 to a partition and block"):
-            nc.gpsimd.dma_start(b_out_cols[:], b_out.rearrange("(a p) o -> p (a o)", p=P))
+        bv_col = held.tile([P, 1], F32, name="bv_col")
         right_mask = held.tile([P, T], F32, name="right_mask")
-        nc.gpsimd.dma_start(right_mask[:], lab.rearrange("o t -> (o t)").partition_broadcast(P))
-        bv_rows = held.tile([P, P], F32, name="bv_rows")
-        nc.gpsimd.dma_start(bv_rows[:], bv.rearrange("e o -> (e o)").partition_broadcast(P))
         wrong_mask = held.tile([P, T], F32, name="wrong_mask")
-        nc.gpsimd.tensor_scalar(wrong_mask[:], right_mask[:], -1.0, 1.0, ALU.mult, ALU.add)
-
         identity = held.tile([P, P], BF16, name="identity")
-        make_identity(nc, identity[:])
         future = held.tile([P, P], BF16, name="future")
+        x_sb = held.tile([P, T], BF16, name="x_sb")
+        q_sb = held.tile([P, T], BF16, name="q_sb")
+        k_sb = held.tile([P, T], BF16, name="k_sb")
+        v_sb = held.tile([P, BLOCKS, P], BF16, name="v_sb")
+        o_sb = held.tile([P, T], BF16, name="o_sb")
+
+        rel_sb, rel_exp, sums, sc_ps, minus_sc, bank_shift, sc_exp = {}, {}, {}, {}, {}, {}, {}
+        inverse, diag, a_ps, a_sb = {}, {}, {}, {}
+
+        def looked_up(piece):
+            return window[:].indirect(offsets[:, piece * (PIECE // 16) : (piece + 1) * (PIECE // 16)])
+
+        def load_rel(i):
+            rel_sb[i] = rel_pool.tile([P, T], F32, name="rel_sb")
+            nc.sync.dma_start(rel_sb[i][:, : (i + 1) * P], rel[i * P : (i + 1) * P, : (i + 1) * P])
+
+        def relation(i):
+            width = (i + 1) * P
+            nc.gpsimd.affine_select(
+                out=rel_sb[i][:, i * P : width], in_=rel_sb[i][:, i * P : width], pattern=[[-1, P]],
+                compare_op=ALU.is_ge, fill=MASKED, base=0, channel_multiplier=1,
+            )
+            rel_shift = work.tile([P, 1], F32, name="rel_shift")
+            nc.vector.tensor_reduce(
+                out=rel_shift[:], in_=rel_sb[i][:, :width], axis=mybir.AxisListType.X, op=ALU.max, negate=True
+            )
+            sums[i] = rel_done.tile([P, 2], F32, name="sums")
+            rel_exp[i] = rel_done.tile([P, T], BF16, name="rel_exp")
+            nc.scalar.activation(
+                rel_exp[i][:, :width], rel_sb[i][:, :width], FUNC.Exp, bias=rel_shift[:, 0:1],
+                accum_out=sums[i][:, 1:2],
+            )
+            if i - LOADS_AHEAD >= 0:
+                load_rel(i - LOADS_AHEAD)
+
+        def scores(i):
+            width = (i + 1) * P
+            sc_ps[i] = []
+            for start in range(0, width, PIECE):
+                w = min(PIECE, width - start)
+                bank = product.tile([P, PIECE], F32, name="sc_ps", tag="product")
+                last = start + w == width
+                nc.tensor.matmul(
+                    bank[:, :w], q_sb[:, i * P : width], k_sb[:, start : start + w], start=True, stop=not last
+                )
+                if last:
+                    nc.tensor.matmul(bank[:, w - P : w], identity[:], future[:], start=False, stop=True)
+                sc_ps[i].append(bank)
+
+        def shift(i):
+            width = (i + 1) * P
+            minus_sc[i] = work.tile([P, T], F32, name="minus_sc")
+            bank_shift[i] = work.tile([P, PER_BANK], F32, name="bank_shift")
+            for c, bank in enumerate(sc_ps[i]):
+                w = min(PIECE, width - c * PIECE)
+                nc.vector.tensor_scalar(
+                    out=minus_sc[i][:, c * PIECE : c * PIECE + w], in0=bank[:, :w], scalar1=-SCALE, scalar2=None,
+                    op0=ALU.mult, op1=ALU.min, accum_out=bank_shift[i][:, c : c + 1],
+                )
+
+        def weigh(i):
+            width = (i + 1) * P
+            sc_shift = work.tile([P, 1], F32, name="sc_shift")
+            nc.vector.tensor_reduce(
+                out=sc_shift[:], in_=bank_shift[i][:, : len(sc_ps[i])], axis=mybir.AxisListType.X, op=ALU.min
+            )
+            sc_exp[i] = work.tile([P, T], BF16, name="sc_exp")
+            nc.scalar.activation(
+                sc_exp[i][:, :width], minus_sc[i][:, :width], FUNC.Exp, bias=sc_shift[:, 0:1], scale=-1.0,
+                accum_out=sums[i][:, 0:1],
+            )
+
+        def invert(i):
+            inverse[i] = work.tile([P, 2], F32, name="inverse")
+            nc.vector.reciprocal(inverse[i][:], sums[i][:])
+
+        def diagonals(i):
+            diag[i] = work.tile([P, 2, P], BF16, name="diag")
+            for part in range(2):
+                nc.gpsimd.tensor_scalar(diag[i][:, part, :], identity[:], inverse[i][:, part : part + 1], None, ALU.mult)
+
+        def flip_weights(i):
+            a_ps[i] = []
+            for first in range(0, i + 1, PER_FLIP):
+                bank = flip.tile([P, PER_FLIP, P], BF16, name="a_ps", tag="flip")
+                for b in range(min(PER_FLIP, i + 1 - first)):
+                    history = slice((first + b) * P, (first + b + 1) * P)
+                    nc.tensor.matmul(bank[:, b, :], sc_exp[i][:, history], diag[i][:, 0, :], start=True, stop=False)
+                    nc.tensor.matmul(bank[:, b, :], rel_exp[i][:, history], diag[i][:, 1, :], start=False, stop=True)
+                a_ps[i].append(bank)
+
+        def keep_weights(i):
+            a_sb[i] = work.tile([P, BLOCKS, P], BF16, name="a_sb")
+            for g, bank in enumerate(a_ps[i]):
+                count = min(PER_FLIP, i + 1 - g * PER_FLIP)
+                nc.vector.tensor_copy(a_sb[i][:, g * PER_FLIP : g * PER_FLIP + count, :], bank[:, :count, :])
+
+        def mix(i):
+            o_ps = mixed.tile([P, PIECE], F32, name="o_ps", tag="mixed")
+            for j in range(i + 1):
+                nc.tensor.matmul(o_ps[:, :P], v_sb[:, j, :], a_sb[i][:, j, :], start=j == 0, stop=j == i)
+            nc.scalar.activation(o_sb[:, i * P : (i + 1) * P], o_ps[:, :P], FUNC.Identity, bias=bv_col[:, 0:1], scale=0.5)
+
+        def project(first, m):
+            cols = slice(first * P, first * P + PIECE)
+            out_ps = product.tile([P, PIECE], F32, name="out_ps", tag="product")
+            nc.tensor.matmul(out_ps[:], weights["out"][:, m * P : (m + 1) * P], o_sb[:, cols], start=True, stop=True)
+            out_sb = store.tile([P, PIECE], F32, name="out_sb")
+            nc.scalar.activation(out_sb[:], out_ps[:], FUNC.Identity, bias=b_out_cols[:, m : m + 1])
+            nc.sync.dma_start(out[m * P : (m + 1) * P, cols], out_sb[:])
+
+        order = list(reversed(range(BLOCKS)))
+
+        make_identity(nc, identity[:])
         nc.gpsimd.memset(future[:], 0.0)
         nc.gpsimd.affine_select(
             out=future[:], in_=future[:], pattern=[[-1, P]], compare_op=ALU.is_ge,
             fill=MASKED, base=0, channel_multiplier=1,
         )
+        nc.sync.dma_start(offsets[:], offs)
+        nc.sync.dma_start(right_mask[:], lab.rearrange("o t -> (o t)").partition_broadcast(P))
+        for i in order[:LOADS_AHEAD]:
+            load_rel(i)
+        nc.scalar.dma_start(table_rows[:], table.rearrange("(a p) d -> p a d", p=P))
+        nc.scalar.dma_start(weights["right"][:], w_right)
+        nc.scalar.dma_start(weights["wrong"][:], w_wrong)
+        nc.scalar.dma_start(b_in_col[:], b_in)
+        nc.scalar.dma_start(weights["q"][:], wq)
+        nc.scalar.dma_start(bq_col[:], bq)
+        nc.scalar.dma_start(weights["k"][:], wk)
+        nc.scalar.dma_start(weights["v"][:], wv)
+        nc.scalar.dma_start(bv_col[:], bv)
+        nc.scalar.dma_start(weights["out"][:], w_out)
+        with nc.allow_non_contiguous_dma(reason="one float32 to a partition and block"):
+            nc.scalar.dma_start(b_out_cols[:], b_out.rearrange("(a p) o -> p (a o)", p=P))
+        nc.gpsimd.tensor_scalar(wrong_mask[:], right_mask[:], -1.0, 1.0, ALU.mult, ALU.add)
 
         flipped = flip.tile([P, ITEMS], BF16, name="flipped", tag="flip")
         for a in range(ITEMS // P):
             nc.tensor.transpose(flipped[:, a * P : (a + 1) * P], table_rows[:, a, :], identity[:])
-        window = held.tile([P, ITEMS], BF16, name="window")
         nc.vector.tensor_copy(window[:], flipped[:])
 
-        def looked_up(piece):
-            return window[:].indirect(offsets[:, piece * (PIECE // 16) : (piece + 1) * (PIECE // 16)])
+        relation(order[0])
 
-        q_sb = held.tile([P, T], BF16, name="q_sb")
+        masked = {}
+        for piece in range(T // PIECE + 1):
+            if piece < T // PIECE:
+                cols = slice(piece * PIECE, (piece + 1) * PIECE)
+                for w_name, mask in (("right", right_mask), ("wrong", wrong_mask)):
+                    x_ps = product.tile([P, PIECE], F32, name="x_ps", tag="product")
+                    nc.tensor.matmul(x_ps[:], weights[w_name][:], looked_up(piece), start=True, stop=True)
+                    masked[w_name, piece] = work.tile([P, PIECE], BF16, name="x_" + w_name)
+                    nc.vector.scalar_tensor_tensor(
+                        out=masked[w_name, piece][:], in0=x_ps[:], scalar=b_in_col[:, 0:1], in1=mask[:, cols],
+                        op0=ALU.add, op1=ALU.mult,
+                    )
+            if piece > 0:
+                nc.vector.tensor_tensor(
+                    x_sb[:, (piece - 1) * PIECE : piece * PIECE], masked["right", piece - 1][:],
+                    masked["wrong", piece - 1][:], ALU.max,
+                )
         for piece in range(T // PIECE):
             cols = slice(piece * PIECE, (piece + 1) * PIECE)
             q_ps = product.tile([P, PIECE], F32, name="q_ps", tag="product")
             nc.tensor.matmul(q_ps[:], weights["q"][:], looked_up(T // PIECE + piece), start=True, stop=True)
             nc.scalar.activation(q_sb[:, cols], q_ps[:], FUNC.Identity, bias=bq_col[:, 0:1])
 
-        x_right = held.tile([P, T], BF16, name="x_right")
-        x_wrong = held.tile([P, T], BF16, name="x_wrong")
-        for piece in range(T // PIECE):
-            cols = slice(piece * PIECE, (piece + 1) * PIECE)
-            for w_name, mask, masked in (("right", right_mask, x_right), ("wrong", wrong_mask, x_wrong)):
-                x_ps = product.tile([P, PIECE], F32, name="x_ps", tag="product")
-                nc.tensor.matmul(x_ps[:], weights[w_name][:], looked_up(piece), start=True, stop=True)
-                nc.vector.scalar_tensor_tensor(
-                    out=masked[:, cols], in0=x_ps[:], scalar=b_in_col[:, 0:1], in1=mask[:, cols],
-                    op0=ALU.add, op1=ALU.mult,
-                )
-        x_sb = held.tile([P, T], BF16, name="x_sb")
-        nc.vector.tensor_tensor(x_sb[:], x_right[:], x_wrong[:], ALU.max)
-
-        k_sb = held.tile([P, T], BF16, name="k_sb")
         for piece in range(T // PIECE):
             cols = slice(piece * PIECE, (piece + 1) * PIECE)
             k_ps = product.tile([P, PIECE], F32, name="k_ps", tag="product")
             nc.tensor.matmul(k_ps[:], weights["k"][:], x_sb[:, cols], start=True, stop=True)
-            nc.vector.tensor_copy(k_sb[:, cols], k_ps[:])
-        v_sb = held.tile([P, BLOCKS, P], BF16, name="v_sb")
+            nc.scalar.copy(k_sb[:, cols], k_ps[:])
+        relation(order[1])
         for first in range(0, BLOCKS, PER_BANK):
             v_ps = product.tile([P, PER_BANK, P], F32, name="v_ps", tag="product")
             for b in range(PER_BANK):
                 j = first + b
                 nc.tensor.matmul(v_ps[:, b, :], x_sb[:, j * P : (j + 1) * P], weights["v"][:], start=True, stop=True)
-            nc.vector.tensor_tensor(
-                v_sb[:, first : first + PER_BANK, :], v_ps[:],
-                bv_rows[:].unsqueeze(1).to_broadcast([P, PER_BANK, P]), ALU.add,
-            )
+            nc.scalar.copy(v_sb[:, first : first + PER_BANK, :], v_ps[:])
 
-        o_sb = held.tile([P, T], BF16, name="o_sb")
-        for i in reversed(range(BLOCKS)):
-            width = (i + 1) * P
-            queries = slice(i * P, width)
-            sums = stats.tile([P, 2], F32, name="sums")
+        def block(n):
+            return order[n] if 0 <= n < BLOCKS else None
 
-            rel_sb = rel_pool.tile([P, T], F32, name="rel_sb")
-            nc.sync.dma_start(rel_sb[:, :width], rel[queries, :width])
-            nc.gpsimd.affine_select(
-                out=rel_sb[:, queries], in_=rel_sb[:, queries], pattern=[[-1, P]], compare_op=ALU.is_ge,
-                fill=MASKED, base=0, channel_multiplier=1,
-            )
-            rel_shift = stats.tile([P, 1], F32, name="rel_shift")
-            nc.vector.tensor_reduce(
-                out=rel_shift[:], in_=rel_sb[:, :width], axis=mybir.AxisListType.X, op=ALU.max, negate=True
-            )
-            rel_exp = rel_exp_pool.tile([P, T], BF16, name="rel_exp")
-            nc.scalar.activation(
-                rel_exp[:, :width], rel_sb[:, :width], FUNC.Exp, bias=rel_shift[:, 0:1], accum_out=sums[:, 1:2]
-            )
-
-            minus_sc = work.tile([P, T], F32, name="minus_sc")
-            sc_shift = stats.tile([P, PER_BANK], F32, name="sc_shift")
-            banks = (width + PIECE - 1) // PIECE
-            for c in range(banks):
-                w = min(PIECE, width - c * PIECE)
-                sc_ps = product.tile([P, PIECE], F32, name="sc_ps", tag="product")
-                last = c == banks - 1
-                nc.tensor.matmul(
-                    sc_ps[:, :w], q_sb[:, queries], k_sb[:, c * PIECE : c * PIECE + w], start=True, stop=not last
-                )
-                if last:
-                    nc.tensor.matmul(sc_ps[:, w - P : w], identity[:], future[:], start=False, stop=True)
-                nc.vector.tensor_scalar(
-                    out=minus_sc[:, c * PIECE : c * PIECE + w], in0=sc_ps[:, :w], scalar1=-SCALE,
-                    scalar2=None if c == 0 else sc_shift[:, c - 1 : c], op0=ALU.mult, op1=ALU.min,
-                    accum_out=sc_shift[:, c : c + 1],
-                )
-            sc_exp = work.tile([P, T], BF16, name="sc_exp")
-            nc.scalar.activation(
-                sc_exp[:, :width], minus_sc[:, :width], FUNC.Exp, bias=sc_shift[:, banks - 1 : banks], scale=-1.0,
-                accum_out=sums[:, 0:1],
-            )
-
-            inverse = stats.tile([P, 2], F32, name="inverse")
-            nc.vector.reciprocal(inverse[:], sums[:])
-            sc_diag = work.tile([P, P], BF16, name="sc_diag")
-            nc.vector.tensor_scalar(sc_diag[:], identity[:], inverse[:, 0:1], None, ALU.mult)
-            rel_diag = work.tile([P, P], BF16, name="rel_diag")
-            nc.vector.tensor_scalar(rel_diag[:], identity[:], inverse[:, 1:2], None, ALU.mult)
-            a_sb = work.tile([P, BLOCKS, P], BF16, name="a_sb")
-            for first in range(0, i + 1, PER_BANK):
-                count = min(PER_BANK, i + 1 - first)
-                a_ps = flip.tile([P, PER_BANK, P], F32, name="a_ps", tag="flip")
-                for b in range(count):
-                    history = slice((first + b) * P, (first + b + 1) * P)
-                    nc.tensor.matmul(a_ps[:, b, :], sc_exp[:, history], sc_diag[:], start=True, stop=False)
-                    nc.tensor.matmul(a_ps[:, b, :], rel_exp[:, history], rel_diag[:], start=False, stop=True)
-                nc.vector.tensor_copy(a_sb[:, first : first + count, :], a_ps[:, :count, :])
-
-            o_ps = mixed.tile([P, P], F32, name="o_ps")
-            for j in range(i + 1):
-                nc.tensor.matmul(o_ps[:], v_sb[:, j, :], a_sb[:, j, :], start=j == 0, stop=j == i)
-            nc.scalar.mul(o_sb[:, queries], o_ps[:], 0.5)
-
-            if i % PER_BANK == 0:
-                cols = slice(i * P, i * P + PIECE)
-                for m in range(OUT // P):
-                    out_ps = product.tile([P, PIECE], F32, name="out_ps", tag="product")
-                    nc.tensor.matmul(out_ps[:], weights["out"][:, m * P : (m + 1) * P], o_sb[:, cols], start=True, stop=True)
-                    out_sb = store.tile([P, PIECE], F32, name="out_sb")
-                    nc.scalar.activation(out_sb[:], out_ps[:], FUNC.Identity, bias=b_out_cols[:, m : m + 1])
-                    nc.gpsimd.dma_start(out[m * P : (m + 1) * P, cols], out_sb[:])
+        scores(order[0])
+        for n in range(BLOCKS + 2):
+            now, after, before, done, ahead = block(n), block(n + 1), block(n - 1), block(n - 2), block(n + REL_AHEAD)
+            if now is not None:
+                shift(now)
+            if after is not None:
+                scores(after)
+            if done is not None:
+                keep_weights(done)
+            if now is not None:
+                weigh(now)
+            if done is not None:
+                mix(done)
+                m = -done % PER_BANK
+                if done + m < BLOCKS:
+                    project(done + m, m)
+            if before is not None:
+                invert(before)
+            if ahead is not None:
+                relation(ahead)
+            if before is not None:
+                diagonals(before)
+                flip_weights(before)
+        for m in range(1, OUT // P):
+            project(0, m)

@@ -48,7 +48,7 @@ def tile_rkt_b_kernel(
         b_in_col = held.tile([P, 1], F32, name="b_in_col")
         bq_col = held.tile([P, 1], F32, name="bq_col")
         b_out_cols = held.tile([P, OUT // P], F32, name="b_out_cols")
-        bv_col = held.tile([P, 1], F32, name="bv_col")
+        bv_rows = held.tile([P, P], F32, name="bv_rows")
         right_mask = held.tile([P, T], F32, name="right_mask")
         wrong_mask = held.tile([P, T], F32, name="wrong_mask")
         identity = held.tile([P, P], BF16, name="identity")
@@ -60,7 +60,7 @@ def tile_rkt_b_kernel(
         o_sb = held.tile([P, T], BF16, name="o_sb")
 
         rel_sb, rel_exp, sums, sc_ps, minus_sc, bank_shift, sc_exp = {}, {}, {}, {}, {}, {}, {}
-        inverse, diag, a_ps, a_sb = {}, {}, {}, {}
+        inverse, diag, a_ps, a_sb, o_ps = {}, {}, {}, {}, {}
 
         def looked_up(piece):
             return window[:].indirect(offsets[:, piece * (PIECE // 16) : (piece + 1) * (PIECE // 16)])
@@ -132,7 +132,7 @@ def tile_rkt_b_kernel(
         def diagonals(i):
             diag[i] = work.tile([P, 2, P], BF16, name="diag")
             for part in range(2):
-                nc.gpsimd.tensor_scalar(diag[i][:, part, :], identity[:], inverse[i][:, part : part + 1], None, ALU.mult)
+                nc.vector.tensor_scalar(diag[i][:, part, :], identity[:], inverse[i][:, part : part + 1], None, ALU.mult)
 
         def flip_weights(i):
             a_ps[i] = []
@@ -151,10 +151,13 @@ def tile_rkt_b_kernel(
                 nc.vector.tensor_copy(a_sb[i][:, g * PER_FLIP : g * PER_FLIP + count, :], bank[:, :count, :])
 
         def mix(i):
-            o_ps = mixed.tile([P, PIECE], F32, name="o_ps", tag="mixed")
+            if i % PER_BANK == PER_BANK - 1:
+                o_ps[0] = mixed.tile([P, PIECE], F32, name="o_ps")
+            cols = slice((i % PER_BANK) * P, (i % PER_BANK + 1) * P)
             for j in range(i + 1):
-                nc.tensor.matmul(o_ps[:, :P], v_sb[:, j, :], a_sb[i][:, j, :], start=j == 0, stop=j == i)
-            nc.scalar.activation(o_sb[:, i * P : (i + 1) * P], o_ps[:, :P], FUNC.Identity, bias=bv_col[:, 0:1], scale=0.5)
+                nc.tensor.matmul(o_ps[0][:, cols], v_sb[:, j, :], a_sb[i][:, j, :], start=j == 0, stop=j == i)
+            if i % PER_BANK == 0:
+                nc.scalar.mul(o_sb[:, i * P : i * P + PIECE], o_ps[0][:], 0.5)
 
         def project(first, m):
             cols = slice(first * P, first * P + PIECE)
@@ -173,10 +176,10 @@ def tile_rkt_b_kernel(
             fill=MASKED, base=0, channel_multiplier=1,
         )
         nc.sync.dma_start(offsets[:], offs)
+        nc.sync.dma_start(table_rows[:], table.rearrange("(a p) d -> p a d", p=P))
         nc.sync.dma_start(right_mask[:], lab.rearrange("o t -> (o t)").partition_broadcast(P))
         for i in order[:LOADS_AHEAD]:
             load_rel(i)
-        nc.scalar.dma_start(table_rows[:], table.rearrange("(a p) d -> p a d", p=P))
         nc.scalar.dma_start(weights["right"][:], w_right)
         nc.scalar.dma_start(weights["wrong"][:], w_wrong)
         nc.scalar.dma_start(b_in_col[:], b_in)
@@ -184,7 +187,7 @@ def tile_rkt_b_kernel(
         nc.scalar.dma_start(bq_col[:], bq)
         nc.scalar.dma_start(weights["k"][:], wk)
         nc.scalar.dma_start(weights["v"][:], wv)
-        nc.scalar.dma_start(bv_col[:], bv)
+        nc.scalar.dma_start(bv_rows[:], bv.rearrange("e o -> (e o)").partition_broadcast(P))
         nc.scalar.dma_start(weights["out"][:], w_out)
         with nc.allow_non_contiguous_dma(reason="one float32 to a partition and block"):
             nc.scalar.dma_start(b_out_cols[:], b_out.rearrange("(a p) o -> p (a o)", p=P))
@@ -231,7 +234,10 @@ def tile_rkt_b_kernel(
             for b in range(PER_BANK):
                 j = first + b
                 nc.tensor.matmul(v_ps[:, b, :], x_sb[:, j * P : (j + 1) * P], weights["v"][:], start=True, stop=True)
-            nc.scalar.copy(v_sb[:, first : first + PER_BANK, :], v_ps[:])
+            nc.vector.tensor_tensor(
+                v_sb[:, first : first + PER_BANK, :], v_ps[:],
+                bv_rows[:].unsqueeze(1).to_broadcast([P, PER_BANK, P]), ALU.add,
+            )
 
         def block(n):
             return order[n] if 0 <= n < BLOCKS else None

@@ -49,8 +49,11 @@ def tile_rkt_b_kernel(
         bq_col = held.tile([P, 1], F32, name="bq_col")
         b_out_cols = held.tile([P, OUT // P], F32, name="b_out_cols")
         bv_rows = held.tile([P, P], F32, name="bv_rows")
-        right_mask = held.tile([P, T], F32, name="right_mask")
-        wrong_mask = held.tile([P, T], F32, name="wrong_mask")
+        lab_row = held.tile([1, T], F32, name="lab_row")
+        lab_bf16 = held.tile([1, T], BF16, name="lab_bf16")
+        ones_row = held.tile([1, P], BF16, name="ones_row")
+        right_mask = held.tile([P, T], BF16, name="right_mask")
+        wrong_mask = held.tile([P, T], BF16, name="wrong_mask")
         identity = held.tile([P, P], BF16, name="identity")
         future = held.tile([P, P], BF16, name="future")
         x_sb = held.tile([P, T], BF16, name="x_sb")
@@ -177,21 +180,29 @@ def tile_rkt_b_kernel(
         )
         nc.sync.dma_start(offsets[:], offs)
         nc.sync.dma_start(table_rows[:], table.rearrange("(a p) d -> p a d", p=P))
-        nc.sync.dma_start(right_mask[:], lab.rearrange("o t -> (o t)").partition_broadcast(P))
         for i in order[:LOADS_AHEAD]:
             load_rel(i)
+        nc.scalar.dma_start(lab_row[:], lab)
         nc.scalar.dma_start(weights["right"][:], w_right)
         nc.scalar.dma_start(weights["wrong"][:], w_wrong)
         nc.scalar.dma_start(b_in_col[:], b_in)
         nc.scalar.dma_start(weights["q"][:], wq)
         nc.scalar.dma_start(bq_col[:], bq)
-        nc.scalar.dma_start(weights["k"][:], wk)
-        nc.scalar.dma_start(weights["v"][:], wv)
-        nc.scalar.dma_start(bv_rows[:], bv.rearrange("e o -> (e o)").partition_broadcast(P))
-        nc.scalar.dma_start(weights["out"][:], w_out)
+        nc.gpsimd.dma_start(weights["k"][:], wk)
+        nc.gpsimd.dma_start(weights["v"][:], wv)
+        nc.gpsimd.dma_start(bv_rows[:], bv.rearrange("e o -> (e o)").partition_broadcast(P))
+        nc.gpsimd.dma_start(weights["out"][:], w_out)
         with nc.allow_non_contiguous_dma(reason="one float32 to a partition and block"):
-            nc.scalar.dma_start(b_out_cols[:], b_out.rearrange("(a p) o -> p (a o)", p=P))
-        nc.gpsimd.tensor_scalar(wrong_mask[:], right_mask[:], -1.0, 1.0, ALU.mult, ALU.add)
+            nc.gpsimd.dma_start(b_out_cols[:], b_out.rearrange("(a p) o -> p (a o)", p=P))
+
+        nc.vector.memset(ones_row[:], 1.0)
+        nc.vector.tensor_copy(lab_bf16[:], lab_row[:])
+        for piece in range(T // PIECE):
+            cols = slice(piece * PIECE, (piece + 1) * PIECE)
+            lab_ps = product.tile([P, PIECE], F32, name="lab_ps", tag="product")
+            nc.tensor.matmul(lab_ps[:], ones_row[:], lab_bf16[:, cols], start=True, stop=True)
+            nc.scalar.copy(right_mask[:, cols], lab_ps[:])
+            nc.vector.tensor_scalar(wrong_mask[:, cols], lab_ps[:], -1.0, 1.0, ALU.mult, ALU.add)
 
         flipped = flip.tile([P, ITEMS], BF16, name="flipped", tag="flip")
         for a in range(ITEMS // P):

@@ -15,8 +15,8 @@ PIECE = 512
 BLOCKS = T // P
 PER_BANK = PIECE // P
 PER_FLIP = 2 * PER_BANK
-LOADS_AHEAD = 4
-REL_AHEAD = 2
+LOADS_AHEAD = 5
+REL_AHEAD = 3
 SCALE = 1.0 / 128.0**0.5
 MASKED = -1.0e30
 
@@ -50,8 +50,10 @@ def tile_rkt_b_kernel(
         b_out_cols = held.tile([P, OUT // P], F32, name="b_out_cols")
         bv_rows = held.tile([P, P], F32, name="bv_rows")
         lab_row = held.tile([1, T], F32, name="lab_row")
-        lab_bf16 = held.tile([1, T], BF16, name="lab_bf16")
-        ones_row = held.tile([1, P], BF16, name="ones_row")
+        lab_bf16 = held.tile([P, T], BF16, name="lab_bf16")
+        ones = held.tile([P, P], BF16, name="ones")
+        bv_row = held.tile([1, P], F32, name="bv_row")
+        ones_row = held.tile([1, P], F32, name="ones_row")
         right_mask = held.tile([P, T], BF16, name="right_mask")
         wrong_mask = held.tile([P, T], BF16, name="wrong_mask")
         identity = held.tile([P, P], BF16, name="identity")
@@ -190,19 +192,20 @@ def tile_rkt_b_kernel(
         nc.scalar.dma_start(bq_col[:], bq)
         nc.gpsimd.dma_start(weights["k"][:], wk)
         nc.gpsimd.dma_start(weights["v"][:], wv)
-        nc.gpsimd.dma_start(bv_rows[:], bv.rearrange("e o -> (e o)").partition_broadcast(P))
+        nc.gpsimd.dma_start(bv_row[:], bv.rearrange("e o -> o e"))
         nc.gpsimd.dma_start(weights["out"][:], w_out)
         with nc.allow_non_contiguous_dma(reason="one float32 to a partition and block"):
             nc.gpsimd.dma_start(b_out_cols[:], b_out.rearrange("(a p) o -> p (a o)", p=P))
 
-        nc.vector.memset(ones_row[:], 1.0)
-        nc.vector.tensor_copy(lab_bf16[:], lab_row[:])
+        nc.vector.memset(ones[:], 1.0)
+        nc.vector.memset(lab_bf16[:], 0.0)
+        nc.vector.tensor_copy(lab_bf16[0:1, :], lab_row[:])
         for piece in range(T // PIECE):
             cols = slice(piece * PIECE, (piece + 1) * PIECE)
             lab_ps = product.tile([P, PIECE], F32, name="lab_ps", tag="product")
-            nc.tensor.matmul(lab_ps[:], ones_row[:], lab_bf16[:, cols], start=True, stop=True)
+            nc.tensor.matmul(lab_ps[:], ones[:], lab_bf16[:, cols], start=True, stop=True)
             nc.scalar.copy(right_mask[:, cols], lab_ps[:])
-            nc.vector.tensor_scalar(wrong_mask[:, cols], lab_ps[:], -1.0, 1.0, ALU.mult, ALU.add)
+            nc.scalar.activation(wrong_mask[:, cols], lab_ps[:], FUNC.Identity, bias=1.0, scale=-1.0)
 
         flipped = flip.tile([P, ITEMS], BF16, name="flipped", tag="flip")
         for a in range(ITEMS // P):
@@ -240,6 +243,11 @@ def tile_rkt_b_kernel(
             nc.tensor.matmul(k_ps[:], weights["k"][:], x_sb[:, cols], start=True, stop=True)
             nc.scalar.copy(k_sb[:, cols], k_ps[:])
         relation(order[1])
+        relation(order[2])
+        nc.vector.memset(ones_row[:], 1.0)
+        bv_ps = product.tile([P, PIECE], F32, name="bv_ps", tag="product")
+        nc.tensor.matmul(bv_ps[:, :P], ones_row[:], bv_row[:], start=True, stop=True)
+        nc.vector.tensor_copy(bv_rows[:], bv_ps[:, :P])
         for first in range(0, BLOCKS, PER_BANK):
             v_ps = product.tile([P, PER_BANK, P], F32, name="v_ps", tag="product")
             for b in range(PER_BANK):

@@ -15,8 +15,8 @@ PIECE = 512
 BLOCKS = T // P
 PER_BANK = PIECE // P
 PER_FLIP = 2 * PER_BANK
-LOADS_AHEAD = 5
-REL_AHEAD = 3
+REL_AHEAD = 1
+RM_PIECE = 512
 SCALE = 1.0 / 128.0**0.5
 MASKED = -1.0e30
 
@@ -31,13 +31,13 @@ def tile_rkt_b_kernel(
     nc = tc.nc
     with ExitStack() as ctx:
         held = ctx.enter_context(tc.tile_pool(name="held", bufs=1))
-        rel_pool = ctx.enter_context(tc.tile_pool(name="rel_pool", bufs=LOADS_AHEAD))
-        rel_done = ctx.enter_context(tc.tile_pool(name="rel_done", bufs=REL_AHEAD + 3))
+        rel_pool = ctx.enter_context(tc.tile_pool(name="rel_pool", bufs=1))
+        rel_done = ctx.enter_context(tc.tile_pool(name="rel_done", bufs=1))
         work = ctx.enter_context(tc.tile_pool(name="work", bufs=3))
         store = ctx.enter_context(tc.tile_pool(name="store", bufs=4))
         product = ctx.enter_context(tc.psum_pool(name="product", bufs=4))
-        flip = ctx.enter_context(tc.psum_pool(name="flip", bufs=2))
-        mixed = ctx.enter_context(tc.psum_pool(name="mixed", bufs=2))
+        flip = ctx.enter_context(tc.psum_pool(name="flip", bufs=3))
+        mixed = ctx.enter_context(tc.psum_pool(name="mixed", bufs=1))
 
         offsets = held.tile([P, 2 * T // 16], U16, name="offsets")
         table_rows = held.tile([P, ITEMS // P, P], BF16, name="table_rows")
@@ -65,14 +65,17 @@ def tile_rkt_b_kernel(
         o_sb = held.tile([P, T], BF16, name="o_sb")
 
         rel_sb, rel_exp, sums, sc_ps, minus_sc, bank_shift, sc_exp = {}, {}, {}, {}, {}, {}, {}
-        inverse, diag, a_ps, a_sb, o_ps = {}, {}, {}, {}, {}
+        inverse, diag, a_ps, a_sb, o_ps, rel_diag = {}, {}, {}, {}, {}, {}
 
         def looked_up(piece):
             return window[:].indirect(offsets[:, piece * (PIECE // 16) : (piece + 1) * (PIECE // 16)])
 
         def load_rel(i):
-            rel_sb[i] = rel_pool.tile([P, T], F32, name="rel_sb")
-            nc.sync.dma_start(rel_sb[i][:, : (i + 1) * P], rel[i * P : (i + 1) * P, : (i + 1) * P])
+            width = (i + 1) * P
+            rel_sb[i] = rel_pool.tile([P, width], F32, name="rel_sb%d" % i)
+            for start in range(0, width, RM_PIECE):
+                cols = slice(start, min(width, start + RM_PIECE))
+                nc.sync.dma_start(rel_sb[i][:, cols], rel[i * P : (i + 1) * P, cols])
 
         def relation(i):
             width = (i + 1) * P
@@ -80,18 +83,27 @@ def tile_rkt_b_kernel(
                 out=rel_sb[i][:, i * P : width], in_=rel_sb[i][:, i * P : width], pattern=[[-1, P]],
                 compare_op=ALU.is_ge, fill=MASKED, base=0, channel_multiplier=1,
             )
+            pieces = -(-width // RM_PIECE)
+            rel_max = work.tile([P, T // RM_PIECE], F32, name="rel_max")
+            for c in range(pieces):
+                nc.vector.tensor_reduce(
+                    out=rel_max[:, c : c + 1], in_=rel_sb[i][:, c * RM_PIECE : min(width, (c + 1) * RM_PIECE)],
+                    axis=mybir.AxisListType.X, op=ALU.max,
+                )
             rel_shift = work.tile([P, 1], F32, name="rel_shift")
             nc.vector.tensor_reduce(
-                out=rel_shift[:], in_=rel_sb[i][:, :width], axis=mybir.AxisListType.X, op=ALU.max, negate=True
+                out=rel_shift[:], in_=rel_max[:, :pieces], axis=mybir.AxisListType.X, op=ALU.max, negate=True
             )
-            sums[i] = rel_done.tile([P, 2], F32, name="sums")
-            rel_exp[i] = rel_done.tile([P, T], BF16, name="rel_exp")
+            rel_sum = rel_done.tile([P, 1], F32, name="rel_sum%d" % i)
+            rel_exp[i] = rel_done.tile([P, (i + 1) * P], BF16, name="rel_exp%d" % i)
             nc.scalar.activation(
                 rel_exp[i][:, :width], rel_sb[i][:, :width], FUNC.Exp, bias=rel_shift[:, 0:1],
-                accum_out=sums[i][:, 1:2],
+                accum_out=rel_sum[:],
             )
-            if i - LOADS_AHEAD >= 0:
-                load_rel(i - LOADS_AHEAD)
+            rel_inverse = rel_done.tile([P, 1], F32, name="rel_inverse%d" % i)
+            nc.vector.reciprocal(rel_inverse[:], rel_sum[:])
+            rel_diag[i] = rel_done.tile([P, P], BF16, name="rel_diag%d" % i)
+            nc.gpsimd.tensor_scalar(rel_diag[i][:], identity[:], rel_inverse[:, 0:1], 0.0, ALU.mult, ALU.add)
 
         def scores(i):
             width = (i + 1) * P
@@ -125,29 +137,36 @@ def tile_rkt_b_kernel(
                 out=sc_shift[:], in_=bank_shift[i][:, : len(sc_ps[i])], axis=mybir.AxisListType.X, op=ALU.min
             )
             sc_exp[i] = work.tile([P, T], BF16, name="sc_exp")
+            sums[i] = work.tile([P, 1], F32, name="sc_sum")
             nc.scalar.activation(
                 sc_exp[i][:, :width], minus_sc[i][:, :width], FUNC.Exp, bias=sc_shift[:, 0:1], scale=-1.0,
                 accum_out=sums[i][:, 0:1],
             )
 
         def invert(i):
-            inverse[i] = work.tile([P, 2], F32, name="inverse")
+            inverse[i] = work.tile([P, 1], F32, name="inverse")
             nc.vector.reciprocal(inverse[i][:], sums[i][:])
 
         def diagonals(i):
-            diag[i] = work.tile([P, 2, P], BF16, name="diag")
-            for part in range(2):
-                nc.vector.tensor_scalar(diag[i][:, part, :], identity[:], inverse[i][:, part : part + 1], None, ALU.mult)
+            diag[i] = work.tile([P, P], BF16, name="diag")
+            nc.vector.tensor_scalar(diag[i][:], identity[:], inverse[i][:, 0:1], None, ALU.mult)
 
-        def flip_weights(i):
+        def flip_relation(i):
             a_ps[i] = []
             for first in range(0, i + 1, PER_FLIP):
                 bank = flip.tile([P, PER_FLIP, P], BF16, name="a_ps", tag="flip")
                 for b in range(min(PER_FLIP, i + 1 - first)):
                     history = slice((first + b) * P, (first + b + 1) * P)
-                    nc.tensor.matmul(bank[:, b, :], sc_exp[i][:, history], diag[i][:, 0, :], start=True, stop=False)
-                    nc.tensor.matmul(bank[:, b, :], rel_exp[i][:, history], diag[i][:, 1, :], start=False, stop=True)
+                    nc.tensor.matmul(bank[:, b, :], rel_exp[i][:, history], rel_diag[i][:], start=b == 0, stop=False)
                 a_ps[i].append(bank)
+
+        def flip_scores(i):
+            for g, bank in enumerate(a_ps[i]):
+                first = g * PER_FLIP
+                count = min(PER_FLIP, i + 1 - first)
+                for b in range(count):
+                    history = slice((first + b) * P, (first + b + 1) * P)
+                    nc.tensor.matmul(bank[:, b, :], sc_exp[i][:, history], diag[i][:], start=False, stop=b == count - 1)
 
         def keep_weights(i):
             a_sb[i] = work.tile([P, BLOCKS, P], BF16, name="a_sb")
@@ -180,16 +199,16 @@ def tile_rkt_b_kernel(
             out=future[:], in_=future[:], pattern=[[-1, P]], compare_op=ALU.is_ge,
             fill=MASKED, base=0, channel_multiplier=1,
         )
+        nc.sync.dma_start(lab_row[:], lab)
+        nc.sync.dma_start(table_rows[:], table.rearrange("(p a) d -> p a d", p=P))
         nc.sync.dma_start(offsets[:], offs)
-        nc.sync.dma_start(table_rows[:], table.rearrange("(a p) d -> p a d", p=P))
-        for i in order[:LOADS_AHEAD]:
-            load_rel(i)
-        nc.scalar.dma_start(lab_row[:], lab)
         nc.scalar.dma_start(weights["right"][:], w_right)
         nc.scalar.dma_start(weights["wrong"][:], w_wrong)
         nc.scalar.dma_start(b_in_col[:], b_in)
         nc.scalar.dma_start(weights["q"][:], wq)
         nc.scalar.dma_start(bq_col[:], bq)
+        for i in order:
+            load_rel(i)
         nc.gpsimd.dma_start(weights["k"][:], wk)
         nc.gpsimd.dma_start(weights["v"][:], wv)
         nc.gpsimd.dma_start(bv_row[:], bv.rearrange("e o -> o e"))
@@ -210,9 +229,9 @@ def tile_rkt_b_kernel(
         flipped = flip.tile([P, ITEMS], BF16, name="flipped", tag="flip")
         for a in range(ITEMS // P):
             nc.tensor.transpose(flipped[:, a * P : (a + 1) * P], table_rows[:, a, :], identity[:])
-        nc.vector.tensor_copy(window[:], flipped[:])
-
-        relation(order[0])
+        nc.vector.tensor_copy(
+            window[:].rearrange("d (p a) -> d p a", p=P), flipped[:].rearrange("d (a p) -> d p a", p=P)
+        )
 
         masked = {}
         for piece in range(T // PIECE + 1):
@@ -242,8 +261,7 @@ def tile_rkt_b_kernel(
             k_ps = product.tile([P, PIECE], F32, name="k_ps", tag="product")
             nc.tensor.matmul(k_ps[:], weights["k"][:], x_sb[:, cols], start=True, stop=True)
             nc.scalar.copy(k_sb[:, cols], k_ps[:])
-        relation(order[1])
-        relation(order[2])
+        relation(order[0])
         nc.vector.memset(ones_row[:], 1.0)
         bv_ps = product.tile([P, PIECE], F32, name="bv_ps", tag="product")
         nc.tensor.matmul(bv_ps[:, :P], ones_row[:], bv_row[:], start=True, stop=True)
@@ -283,6 +301,8 @@ def tile_rkt_b_kernel(
                 relation(ahead)
             if before is not None:
                 diagonals(before)
-                flip_weights(before)
+                flip_scores(before)
+            if now is not None:
+                flip_relation(now)
         for m in range(1, OUT // P):
             project(0, m)

@@ -48,12 +48,10 @@ def tile_rkt_b_kernel(
         b_in_col = held.tile([P, 1], F32, name="b_in_col")
         bq_col = held.tile([P, 1], F32, name="bq_col")
         b_out_cols = held.tile([P, OUT // P], F32, name="b_out_cols")
-        bv_rows = held.tile([P, P], F32, name="bv_rows")
+        bv_col = held.tile([P, 1], F32, name="bv_col")
         lab_row = held.tile([1, T], F32, name="lab_row")
         lab_bf16 = held.tile([P, T], BF16, name="lab_bf16")
         ones = held.tile([P, P], BF16, name="ones")
-        bv_row = held.tile([1, P], F32, name="bv_row")
-        ones_row = held.tile([1, P], F32, name="ones_row")
         right_mask = held.tile([P, T], BF16, name="right_mask")
         wrong_mask = held.tile([P, T], BF16, name="wrong_mask")
         identity = held.tile([P, P], BF16, name="identity")
@@ -70,11 +68,14 @@ def tile_rkt_b_kernel(
         def looked_up(piece):
             return window[:].indirect(offsets[:, piece * (PIECE // 16) : (piece + 1) * (PIECE // 16)])
 
+        def rel_piece(i):
+            return RM_PIECE if i in order[:2] else (i + 1) * P
+
         def load_rel(i):
             width = (i + 1) * P
             rel_sb[i] = rel_pool.tile([P, width], F32, name="rel_sb%d" % i)
-            for start in range(0, width, RM_PIECE):
-                cols = slice(start, min(width, start + RM_PIECE))
+            for start in range(0, width, rel_piece(i)):
+                cols = slice(start, min(width, start + rel_piece(i)))
                 nc.sync.dma_start(rel_sb[i][:, cols], rel[i * P : (i + 1) * P, cols])
 
         def relation(i):
@@ -83,17 +84,17 @@ def tile_rkt_b_kernel(
                 out=rel_sb[i][:, i * P : width], in_=rel_sb[i][:, i * P : width], pattern=[[-1, P]],
                 compare_op=ALU.is_ge, fill=MASKED, base=0, channel_multiplier=1,
             )
-            pieces = -(-width // RM_PIECE)
-            rel_max = work.tile([P, T // RM_PIECE], F32, name="rel_max")
-            for c in range(pieces):
-                nc.vector.tensor_reduce(
-                    out=rel_max[:, c : c + 1], in_=rel_sb[i][:, c * RM_PIECE : min(width, (c + 1) * RM_PIECE)],
-                    axis=mybir.AxisListType.X, op=ALU.max,
-                )
+            pieces = -(-width // rel_piece(i))
+            rel_max = rel_sb[i]
+            if pieces > 1:
+                rel_max = work.tile([P, pieces], F32, name="rel_max")
+                for c in range(pieces):
+                    nc.vector.tensor_reduce(
+                        out=rel_max[:, c : c + 1], in_=rel_sb[i][:, c * RM_PIECE : min(width, (c + 1) * RM_PIECE)],
+                        axis=mybir.AxisListType.X, op=ALU.max,
+                    )
             rel_shift = work.tile([P, 1], F32, name="rel_shift")
-            nc.vector.tensor_reduce(
-                out=rel_shift[:], in_=rel_max[:, :pieces], axis=mybir.AxisListType.X, op=ALU.max, negate=True
-            )
+            nc.vector.tensor_reduce(out=rel_shift[:], in_=rel_max[:], axis=mybir.AxisListType.X, op=ALU.max, negate=True)
             rel_sum = rel_done.tile([P, 1], F32, name="rel_sum%d" % i)
             rel_exp[i] = rel_done.tile([P, (i + 1) * P], BF16, name="rel_exp%d" % i)
             nc.scalar.activation(
@@ -181,7 +182,9 @@ def tile_rkt_b_kernel(
             for j in range(i + 1):
                 nc.tensor.matmul(o_ps[0][:, cols], v_sb[:, j, :], a_sb[i][:, j, :], start=j == 0, stop=j == i)
             if i % PER_BANK == 0:
-                nc.scalar.mul(o_sb[:, i * P : i * P + PIECE], o_ps[0][:], 0.5)
+                nc.scalar.activation(
+                    o_sb[:, i * P : i * P + PIECE], o_ps[0][:], FUNC.Identity, bias=bv_col[:, 0:1], scale=0.5
+                )
 
         def project(first, m):
             cols = slice(first * P, first * P + PIECE)
@@ -211,7 +214,7 @@ def tile_rkt_b_kernel(
             load_rel(i)
         nc.gpsimd.dma_start(weights["k"][:], wk)
         nc.gpsimd.dma_start(weights["v"][:], wv)
-        nc.gpsimd.dma_start(bv_row[:], bv.rearrange("e o -> o e"))
+        nc.gpsimd.dma_start(bv_col[:], bv)
         nc.gpsimd.dma_start(weights["out"][:], w_out)
         with nc.allow_non_contiguous_dma(reason="one float32 to a partition and block"):
             nc.gpsimd.dma_start(b_out_cols[:], b_out.rearrange("(a p) o -> p (a o)", p=P))
@@ -262,19 +265,12 @@ def tile_rkt_b_kernel(
             nc.tensor.matmul(k_ps[:], weights["k"][:], x_sb[:, cols], start=True, stop=True)
             nc.scalar.copy(k_sb[:, cols], k_ps[:])
         relation(order[0])
-        nc.vector.memset(ones_row[:], 1.0)
-        bv_ps = product.tile([P, PIECE], F32, name="bv_ps", tag="product")
-        nc.tensor.matmul(bv_ps[:, :P], ones_row[:], bv_row[:], start=True, stop=True)
-        nc.vector.tensor_copy(bv_rows[:], bv_ps[:, :P])
-        for first in range(0, BLOCKS, PER_BANK):
-            v_ps = product.tile([P, PER_BANK, P], F32, name="v_ps", tag="product")
-            for b in range(PER_BANK):
+        for first in range(0, BLOCKS, PER_FLIP):
+            v_ps = product.tile([P, PER_FLIP, P], BF16, name="v_ps", tag="product")
+            for b in range(PER_FLIP):
                 j = first + b
                 nc.tensor.matmul(v_ps[:, b, :], x_sb[:, j * P : (j + 1) * P], weights["v"][:], start=True, stop=True)
-            nc.vector.tensor_tensor(
-                v_sb[:, first : first + PER_BANK, :], v_ps[:],
-                bv_rows[:].unsqueeze(1).to_broadcast([P, PER_BANK, P]), ALU.add,
-            )
+            nc.vector.tensor_copy(v_sb[:, first : first + PER_FLIP, :], v_ps[:])
 
         def block(n):
             return order[n] if 0 <= n < BLOCKS else None

@@ -203,7 +203,7 @@ def tile_rkt_b_kernel(
             fill=MASKED, base=0, channel_multiplier=1,
         )
         nc.sync.dma_start(lab_row[:], lab)
-        nc.sync.dma_start(table_rows[:], table.rearrange("(p a) d -> p a d", p=P))
+        nc.sync.dma_start(table_rows[:], table.rearrange("(a p) d -> p a d", p=P))
         nc.sync.dma_start(offsets[:], offs)
         nc.scalar.dma_start(weights["right"][:], w_right)
         nc.scalar.dma_start(weights["wrong"][:], w_wrong)
@@ -232,9 +232,7 @@ def tile_rkt_b_kernel(
         flipped = flip.tile([P, ITEMS], BF16, name="flipped", tag="flip")
         for a in range(ITEMS // P):
             nc.tensor.transpose(flipped[:, a * P : (a + 1) * P], table_rows[:, a, :], identity[:])
-        nc.vector.tensor_copy(
-            window[:].rearrange("d (p a) -> d p a", p=P), flipped[:].rearrange("d (a p) -> d p a", p=P)
-        )
+        nc.vector.tensor_copy(window[:], flipped[:])
 
         masked = {}
         for piece in range(T // PIECE + 1):

@@ -234,23 +234,17 @@ def tile_rkt_b_kernel(
             nc.tensor.transpose(flipped[:, a * P : (a + 1) * P], table_rows[:, a, :], identity[:])
         nc.vector.tensor_copy(window[:], flipped[:])
 
-        masked = {}
-        for piece in range(T // PIECE + 1):
-            if piece < T // PIECE:
-                cols = slice(piece * PIECE, (piece + 1) * PIECE)
-                for w_name, mask in (("right", right_mask), ("wrong", wrong_mask)):
-                    x_ps = product.tile([P, PIECE], F32, name="x_ps", tag="product")
-                    nc.tensor.matmul(x_ps[:], weights[w_name][:], looked_up(piece), start=True, stop=True)
-                    masked[w_name, piece] = work.tile([P, PIECE], BF16, name="x_" + w_name)
-                    nc.vector.scalar_tensor_tensor(
-                        out=masked[w_name, piece][:], in0=x_ps[:], scalar=b_in_col[:, 0:1], in1=mask[:, cols],
-                        op0=ALU.add, op1=ALU.mult,
-                    )
-            if piece > 0:
-                nc.vector.tensor_tensor(
-                    x_sb[:, (piece - 1) * PIECE : piece * PIECE], masked["right", piece - 1][:],
-                    masked["wrong", piece - 1][:], ALU.max,
-                )
+        for piece in range(T // PIECE):
+            cols = slice(piece * PIECE, (piece + 1) * PIECE)
+            masked = {}
+            for w_name, mask in (("right", right_mask), ("wrong", wrong_mask)):
+                x_ps = product.tile([P, PIECE], F32, name="x_ps", tag="product")
+                nc.tensor.matmul(x_ps[:], weights[w_name][:], looked_up(piece), start=True, stop=True)
+                relu = work.tile([P, PIECE], BF16, name="relu_" + w_name)
+                nc.scalar.activation(relu[:], x_ps[:], FUNC.Relu, bias=b_in_col[:, 0:1])
+                masked[w_name] = work.tile([P, PIECE], BF16, name="x_" + w_name)
+                nc.vector.tensor_tensor(masked[w_name][:], relu[:], mask[:, cols], ALU.mult)
+            nc.vector.tensor_tensor(x_sb[:, cols], masked["right"][:], masked["wrong"][:], ALU.max)
         for piece in range(T // PIECE):
             cols = slice(piece * PIECE, (piece + 1) * PIECE)
             q_ps = product.tile([P, PIECE], F32, name="q_ps", tag="product")

@@ -15,7 +15,6 @@ PIECE = 512
 BLOCKS = T // P
 PER_BANK = PIECE // P
 PER_FLIP = 2 * PER_BANK
-REL_AHEAD = 1
 RM_PIECE = 512
 SCALE = 1.0 / 128.0**0.5
 MASKED = -1.0e30
@@ -52,8 +51,6 @@ def tile_rkt_b_kernel(
         lab_row = held.tile([1, T], F32, name="lab_row")
         lab_bf16 = held.tile([P, T], BF16, name="lab_bf16")
         ones = held.tile([P, P], BF16, name="ones")
-        right_mask = held.tile([P, T], BF16, name="right_mask")
-        wrong_mask = held.tile([P, T], BF16, name="wrong_mask")
         identity = held.tile([P, P], BF16, name="identity")
         future = held.tile([P, P], BF16, name="future")
         x_sb = held.tile([P, T], BF16, name="x_sb")
@@ -78,7 +75,7 @@ def tile_rkt_b_kernel(
                 cols = slice(start, min(width, start + rel_piece(i)))
                 nc.sync.dma_start(rel_sb[i][:, cols], rel[i * P : (i + 1) * P, cols])
 
-        def relation(i):
+        def relation(i, rel_sum):
             width = (i + 1) * P
             nc.gpsimd.affine_select(
                 out=rel_sb[i][:, i * P : width], in_=rel_sb[i][:, i * P : width], pattern=[[-1, P]],
@@ -95,16 +92,11 @@ def tile_rkt_b_kernel(
                     )
             rel_shift = work.tile([P, 1], F32, name="rel_shift")
             nc.vector.tensor_reduce(out=rel_shift[:], in_=rel_max[:], axis=mybir.AxisListType.X, op=ALU.max, negate=True)
-            rel_sum = rel_done.tile([P, 1], F32, name="rel_sum%d" % i)
             rel_exp[i] = rel_done.tile([P, (i + 1) * P], BF16, name="rel_exp%d" % i)
             nc.scalar.activation(
                 rel_exp[i][:, :width], rel_sb[i][:, :width], FUNC.Exp, bias=rel_shift[:, 0:1],
-                accum_out=rel_sum[:],
+                accum_out=rel_sum,
             )
-            rel_inverse = rel_done.tile([P, 1], F32, name="rel_inverse%d" % i)
-            nc.vector.reciprocal(rel_inverse[:], rel_sum[:])
-            rel_diag[i] = rel_done.tile([P, P], BF16, name="rel_diag%d" % i)
-            nc.gpsimd.tensor_scalar(rel_diag[i][:], identity[:], rel_inverse[:, 0:1], 0.0, ALU.mult, ALU.add)
 
         def scores(i):
             width = (i + 1) * P
@@ -131,26 +123,32 @@ def tile_rkt_b_kernel(
                     op0=ALU.mult, op1=ALU.min, accum_out=bank_shift[i][:, c : c + 1],
                 )
 
-        def weigh(i):
+        def weigh(i, sc_sum):
             width = (i + 1) * P
             sc_shift = work.tile([P, 1], F32, name="sc_shift")
             nc.vector.tensor_reduce(
                 out=sc_shift[:], in_=bank_shift[i][:, : len(sc_ps[i])], axis=mybir.AxisListType.X, op=ALU.min
             )
             sc_exp[i] = work.tile([P, T], BF16, name="sc_exp")
-            sums[i] = work.tile([P, 1], F32, name="sc_sum")
             nc.scalar.activation(
                 sc_exp[i][:, :width], minus_sc[i][:, :width], FUNC.Exp, bias=sc_shift[:, 0:1], scale=-1.0,
-                accum_out=sums[i][:, 0:1],
+                accum_out=sc_sum,
             )
 
-        def invert(i):
-            inverse[i] = work.tile([P, 1], F32, name="inverse")
-            nc.vector.reciprocal(inverse[i][:], sums[i][:])
+        def invert(n):
+            cols = slice(0 if block(n) is not None else 1, 2 if block(n + 1) is not None else 1)
+            inverse[n] = work.tile([P, 2], F32, name="inverse")
+            nc.vector.reciprocal(inverse[n][:, cols], sums[n][:, cols])
 
-        def diagonals(i):
-            diag[i] = work.tile([P, P], BF16, name="diag")
-            nc.vector.tensor_scalar(diag[i][:], identity[:], inverse[i][:, 0:1], None, ALU.mult)
+        def diagonals(n):
+            if block(n) is not None:
+                diag[block(n)] = work.tile([P, P], BF16, name="diag")
+                nc.gpsimd.tensor_scalar(diag[block(n)][:], identity[:], inverse[n][:, 0:1], 0.0, ALU.mult, ALU.add)
+            if block(n + 1) is not None:
+                rel_diag[block(n + 1)] = rel_done.tile([P, P], BF16, name="rel_diag%d" % block(n + 1))
+                nc.gpsimd.tensor_scalar(
+                    rel_diag[block(n + 1)][:], identity[:], inverse[n][:, 1:2], 0.0, ALU.mult, ALU.add
+                )
 
         def flip_relation(i):
             a_ps[i] = []
@@ -181,7 +179,11 @@ def tile_rkt_b_kernel(
             cols = slice((i % PER_BANK) * P, (i % PER_BANK + 1) * P)
             for j in range(i + 1):
                 nc.tensor.matmul(o_ps[0][:, cols], v_sb[:, j, :], a_sb[i][:, j, :], start=j == 0, stop=j == i)
-            if i % PER_BANK == 0:
+            if i < PER_BANK:
+                nc.scalar.activation(
+                    o_sb[:, i * P : (i + 1) * P], o_ps[0][:, cols], FUNC.Identity, bias=bv_col[:, 0:1], scale=0.5
+                )
+            elif i % PER_BANK == 0:
                 nc.scalar.activation(
                     o_sb[:, i * P : i * P + PIECE], o_ps[0][:], FUNC.Identity, bias=bv_col[:, 0:1], scale=0.5
                 )
@@ -194,7 +196,21 @@ def tile_rkt_b_kernel(
             nc.scalar.activation(out_sb[:], out_ps[:], FUNC.Identity, bias=b_out_cols[:, m : m + 1])
             nc.sync.dma_start(out[m * P : (m + 1) * P, cols], out_sb[:])
 
+        def project_block(i):
+            cols = slice(i * P, (i + 1) * P)
+            out_ps = product.tile([P, OUT // P, P], F32, name="out_ps", tag="product")
+            for m in range(OUT // P):
+                nc.tensor.matmul(out_ps[:, m, :], weights["out"][:, m * P : (m + 1) * P], o_sb[:, cols], start=True, stop=True)
+            out_sb = store.tile([P, OUT // P, P], F32, name="out_sb")
+            nc.vector.tensor_tensor(
+                out_sb[:], out_ps[:], b_out_cols[:].unsqueeze(2).to_broadcast([P, OUT // P, P]), ALU.add
+            )
+            nc.sync.dma_start(out.rearrange("(m p) q -> p m q", p=P)[:, :, cols], out_sb[:])
+
         order = list(reversed(range(BLOCKS)))
+
+        def block(n):
+            return order[n] if 0 <= n < BLOCKS else None
 
         make_identity(nc, identity[:])
         nc.gpsimd.memset(future[:], 0.0)
@@ -220,14 +236,12 @@ def tile_rkt_b_kernel(
             nc.gpsimd.dma_start(b_out_cols[:], b_out.rearrange("(a p) o -> p (a o)", p=P))
 
         nc.vector.memset(ones[:], 1.0)
-        nc.vector.memset(lab_bf16[:], 0.0)
-        nc.vector.tensor_copy(lab_bf16[0:1, :], lab_row[:])
+        nc.vector.memset(lab_bf16[:].bitcast(F32), 0.0)
+        lab_ps = [flip.tile([P, 2, PIECE], BF16, name="lab_ps%d" % h, tag="flip") for h in range(T // PIECE // 2)]
         for piece in range(T // PIECE):
             cols = slice(piece * PIECE, (piece + 1) * PIECE)
-            lab_ps = product.tile([P, PIECE], F32, name="lab_ps", tag="product")
-            nc.tensor.matmul(lab_ps[:], ones[:], lab_bf16[:, cols], start=True, stop=True)
-            nc.scalar.copy(right_mask[:, cols], lab_ps[:])
-            nc.scalar.activation(wrong_mask[:, cols], lab_ps[:], FUNC.Identity, bias=1.0, scale=-1.0)
+            nc.vector.tensor_copy(lab_bf16[0:1, cols], lab_row[:, cols])
+            nc.tensor.matmul(lab_ps[piece // 2][:, piece % 2, :], ones[:], lab_bf16[:, cols], start=True, stop=True)
 
         flipped = flip.tile([P, ITEMS], BF16, name="flipped", tag="flip")
         for a in range(ITEMS // P):
@@ -236,14 +250,18 @@ def tile_rkt_b_kernel(
 
         for piece in range(T // PIECE):
             cols = slice(piece * PIECE, (piece + 1) * PIECE)
-            masked = {}
-            for w_name, mask in (("right", right_mask), ("wrong", wrong_mask)):
+            relu, masked = {}, {}
+            for w_name in ("right", "wrong"):
                 x_ps = product.tile([P, PIECE], F32, name="x_ps", tag="product")
                 nc.tensor.matmul(x_ps[:], weights[w_name][:], looked_up(piece), start=True, stop=True)
-                relu = work.tile([P, PIECE], BF16, name="relu_" + w_name)
-                nc.scalar.activation(relu[:], x_ps[:], FUNC.Relu, bias=b_in_col[:, 0:1])
+                relu[w_name] = work.tile([P, PIECE], BF16, name="relu_" + w_name)
+                nc.scalar.activation(relu[w_name][:], x_ps[:], FUNC.Relu, bias=b_in_col[:, 0:1])
                 masked[w_name] = work.tile([P, PIECE], BF16, name="x_" + w_name)
-                nc.vector.tensor_tensor(masked[w_name][:], relu[:], mask[:, cols], ALU.mult)
+            lab_piece = lab_ps[piece // 2][:, piece % 2, :]
+            nc.vector.tensor_tensor(masked["right"][:], relu["right"][:], lab_piece, ALU.mult)
+            nc.vector.scalar_tensor_tensor(
+                out=masked["wrong"][:], in0=lab_piece, scalar=0.0, in1=relu["wrong"][:], op0=ALU.is_equal, op1=ALU.mult
+            )
             nc.vector.tensor_tensor(x_sb[:, cols], masked["right"][:], masked["wrong"][:], ALU.max)
         for piece in range(T // PIECE):
             cols = slice(piece * PIECE, (piece + 1) * PIECE)
@@ -256,7 +274,10 @@ def tile_rkt_b_kernel(
             k_ps = product.tile([P, PIECE], F32, name="k_ps", tag="product")
             nc.tensor.matmul(k_ps[:], weights["k"][:], x_sb[:, cols], start=True, stop=True)
             nc.scalar.copy(k_sb[:, cols], k_ps[:])
-        relation(order[0])
+        sums[-1] = work.tile([P, 2], F32, name="sums")
+        relation(order[0], sums[-1][:, 1:2])
+        invert(-1)
+        diagonals(-1)
         for first in range(0, BLOCKS, PER_FLIP):
             v_ps = product.tile([P, PER_FLIP, P], BF16, name="v_ps", tag="product")
             for b in range(PER_FLIP):
@@ -264,12 +285,9 @@ def tile_rkt_b_kernel(
                 nc.tensor.matmul(v_ps[:, b, :], x_sb[:, j * P : (j + 1) * P], weights["v"][:], start=True, stop=True)
             nc.vector.tensor_copy(v_sb[:, first : first + PER_FLIP, :], v_ps[:])
 
-        def block(n):
-            return order[n] if 0 <= n < BLOCKS else None
-
         scores(order[0])
         for n in range(BLOCKS + 2):
-            now, after, before, done, ahead = block(n), block(n + 1), block(n - 1), block(n - 2), block(n + REL_AHEAD)
+            now, after, before, done = block(n), block(n + 1), block(n - 1), block(n - 2)
             if now is not None:
                 shift(now)
             if after is not None:
@@ -277,20 +295,21 @@ def tile_rkt_b_kernel(
             if done is not None:
                 keep_weights(done)
             if now is not None:
-                weigh(now)
+                sums[n] = work.tile([P, 2], F32, name="sums")
+                weigh(now, sums[n][:, 0:1])
             if done is not None:
                 mix(done)
                 m = -done % PER_BANK
-                if done + m < BLOCKS:
+                if PER_BANK <= done + m < BLOCKS:
                     project(done + m, m)
+                if done < PER_BANK:
+                    project_block(done)
             if before is not None:
-                invert(before)
-            if ahead is not None:
-                relation(ahead)
+                invert(n - 1)
+            if after is not None:
+                relation(after, sums[n][:, 1:2])
             if before is not None:
-                diagonals(before)
+                diagonals(n - 1)
                 flip_scores(before)
             if now is not None:
                 flip_relation(now)
-        for m in range(1, OUT // P):
-            project(0, m)

@@ -125,10 +125,12 @@ def tile_rkt_b_kernel(
 
         def weigh(i, sc_sum):
             width = (i + 1) * P
-            sc_shift = work.tile([P, 1], F32, name="sc_shift")
-            nc.vector.tensor_reduce(
-                out=sc_shift[:], in_=bank_shift[i][:, : len(sc_ps[i])], axis=mybir.AxisListType.X, op=ALU.min
-            )
+            sc_shift = bank_shift[i]
+            if len(sc_ps[i]) > 1:
+                sc_shift = work.tile([P, 1], F32, name="sc_shift")
+                nc.vector.tensor_reduce(
+                    out=sc_shift[:], in_=bank_shift[i][:, : len(sc_ps[i])], axis=mybir.AxisListType.X, op=ALU.min
+                )
             sc_exp[i] = work.tile([P, T], BF16, name="sc_exp")
             nc.scalar.activation(
                 sc_exp[i][:, :width], minus_sc[i][:, :width], FUNC.Exp, bias=sc_shift[:, 0:1], scale=-1.0,

from contextlib import ExitStack

import concourse.mybir as mybir
from concourse.masks import make_identity

BF16, F32, U16 = mybir.dt.bfloat16, mybir.dt.float32, mybir.dt.uint16
ALU = mybir.AluOpType
FUNC = mybir.ActivationFunctionType

P = 128
ITEMS = 1024
T = 2048
OUT = 512
PIECE = 512
BLOCKS = T // P
PER_BANK = PIECE // P
PER_FLIP = 2 * PER_BANK
RM_PIECE = 512
SCALE = 1.0 / 128.0**0.5
MASKED = -1.0e30

PAIRS = T * (T + 1) // 2
FLOPS = 2 * P * (3 * P * T + 2 * P * T + 2 * PAIRS + OUT * T)
BYTES = 4 * PAIRS + 4 * OUT * T + 2 * ITEMS * P + 2 * P * (5 * P + OUT) + 2 * 2 * T + 4 * T


def tile_rkt_b_kernel(
    tc, table, w_right, w_wrong, b_in, lab, wq, bq, wk, wv, bv, rel, w_out, b_out, offs, out
):
    nc = tc.nc
    with ExitStack() as ctx:
        held = ctx.enter_context(tc.tile_pool(name="held", bufs=1))
        rel_pool = ctx.enter_context(tc.tile_pool(name="rel_pool", bufs=1))
        rel_done = ctx.enter_context(tc.tile_pool(name="rel_done", bufs=1))
        work = ctx.enter_context(tc.tile_pool(name="work", bufs=3))
        store = ctx.enter_context(tc.tile_pool(name="store", bufs=4))
        product = ctx.enter_context(tc.psum_pool(name="product", bufs=4))
        flip = ctx.enter_context(tc.psum_pool(name="flip", bufs=3))
        mixed = ctx.enter_context(tc.psum_pool(name="mixed", bufs=1))

        offsets = held.tile([P, 2 * T // 16], U16, name="offsets")
        table_rows = held.tile([P, ITEMS // P, P], BF16, name="table_rows")
        window = held.tile([P, ITEMS], BF16, name="window")
        weights = {}
        for name, w in (("right", w_right), ("wrong", w_wrong), ("q", wq), ("k", wk), ("v", wv), ("out", w_out)):
            weights[name] = held.tile([P, w.shape[1]], BF16, name="w_" + name)
        b_in_col = held.tile([P, 1], F32, name="b_in_col")
        bq_col = held.tile([P, 1], F32, name="bq_col")
        b_out_cols = held.tile([P, OUT // P], F32, name="b_out_cols")
        bv_col = held.tile([P, 1], F32, name="bv_col")
        lab_row = held.tile([1, T], F32, name="lab_row")
        lab_bf16 = held.tile([P, T], BF16, name="lab_bf16")
        ones = held.tile([P, P], BF16, name="ones")
        identity = held.tile([P, P], BF16, name="identity")
        future = held.tile([P, P], BF16, name="future")
        x_sb = held.tile([P, T], BF16, name="x_sb")
        q_sb = held.tile([P, T], BF16, name="q_sb")
        k_sb = held.tile([P, T], BF16, name="k_sb")
        v_sb = held.tile([P, BLOCKS, P], BF16, name="v_sb")
        o_sb = held.tile([P, T], BF16, name="o_sb")

        rel_sb, rel_exp, sums, sc_ps, minus_sc, bank_shift, sc_exp = {}, {}, {}, {}, {}, {}, {}
        inverse, diag, a_ps, a_sb, o_ps, rel_diag = {}, {}, {}, {}, {}, {}

        def looked_up(piece):
            return window[:].indirect(offsets[:, piece * (PIECE // 16) : (piece + 1) * (PIECE // 16)])

        def rel_piece(i):
            return RM_PIECE if i in order[:2] else (i + 1) * P

        def load_rel(i):
            width = (i + 1) * P
            rel_sb[i] = rel_pool.tile([P, width], F32, name="rel_sb%d" % i)
            for start in range(0, width, rel_piece(i)):
                cols = slice(start, min(width, start + rel_piece(i)))
                nc.sync.dma_start(rel_sb[i][:, cols], rel[i * P : (i + 1) * P, cols])

        def relation(i, rel_sum):
            width = (i + 1) * P
            nc.gpsimd.affine_select(
                out=rel_sb[i][:, i * P : width], in_=rel_sb[i][:, i * P : width], pattern=[[-1, P]],
                compare_op=ALU.is_ge, fill=MASKED, base=0, channel_multiplier=1,
            )
            pieces = -(-width // rel_piece(i))
            rel_max = rel_sb[i]
            if pieces > 1:
                rel_max = work.tile([P, pieces], F32, name="rel_max")
                for c in range(pieces):
                    nc.vector.tensor_reduce(
                        out=rel_max[:, c : c + 1], in_=rel_sb[i][:, c * RM_PIECE : min(width, (c + 1) * RM_PIECE)],
                        axis=mybir.AxisListType.X, op=ALU.max,
                    )
            rel_shift = work.tile([P, 1], F32, name="rel_shift")
            nc.vector.tensor_reduce(out=rel_shift[:], in_=rel_max[:], axis=mybir.AxisListType.X, op=ALU.max, negate=True)
            rel_exp[i] = rel_done.tile([P, (i + 1) * P], BF16, name="rel_exp%d" % i)
            nc.scalar.activation(
                rel_exp[i][:, :width], rel_sb[i][:, :width], FUNC.Exp, bias=rel_shift[:, 0:1],
                accum_out=rel_sum,
            )

        def scores(i):
            width = (i + 1) * P
            sc_ps[i] = []
            for start in range(0, width, PIECE):
                w = min(PIECE, width - start)
                bank = product.tile([P, PIECE], F32, name="sc_ps", tag="product")
                last = start + w == width
                nc.tensor.matmul(
                    bank[:, :w], q_sb[:, i * P : width], k_sb[:, start : start + w], start=True, stop=not last
                )
                if last:
                    nc.tensor.matmul(bank[:, w - P : w], identity[:], future[:], start=False, stop=True)
                sc_ps[i].append(bank)

        def shift(i):
            width = (i + 1) * P
            minus_sc[i] = work.tile([P, T], F32, name="minus_sc")
            bank_shift[i] = work.tile([P, PER_BANK], F32, name="bank_shift")
            for c, bank in enumerate(sc_ps[i]):
                w = min(PIECE, width - c * PIECE)
                nc.vector.tensor_scalar(
                    out=minus_sc[i][:, c * PIECE : c * PIECE + w], in0=bank[:, :w], scalar1=-SCALE, scalar2=None,
                    op0=ALU.mult, op1=ALU.min, accum_out=bank_shift[i][:, c : c + 1],
                )

        def weigh(i, sc_sum):
            width = (i + 1) * P
            sc_shift = bank_shift[i]
            if len(sc_ps[i]) > 1:
                sc_shift = work.tile([P, 1], F32, name="sc_shift")
                nc.vector.tensor_reduce(
                    out=sc_shift[:], in_=bank_shift[i][:, : len(sc_ps[i])], axis=mybir.AxisListType.X, op=ALU.min
                )
            sc_exp[i] = work.tile([P, T], BF16, name="sc_exp")
            nc.scalar.activation(
                sc_exp[i][:, :width], minus_sc[i][:, :width], FUNC.Exp, bias=sc_shift[:, 0:1], scale=-1.0,
                accum_out=sc_sum,
            )

        def invert(n):
            cols = slice(0 if block(n) is not None else 1, 2 if block(n + 1) is not None else 1)
            inverse[n] = work.tile([P, 2], F32, name="inverse")
            nc.vector.reciprocal(inverse[n][:, cols], sums[n][:, cols])

        def diagonals(n):
            if block(n) is not None:
                diag[block(n)] = work.tile([P, P], BF16, name="diag")
                nc.gpsimd.tensor_scalar(diag[block(n)][:], identity[:], inverse[n][:, 0:1], 0.0, ALU.mult, ALU.add)
            if block(n + 1) is not None:
                rel_diag[block(n + 1)] = rel_done.tile([P, P], BF16, name="rel_diag%d" % block(n + 1))
                nc.gpsimd.tensor_scalar(
                    rel_diag[block(n + 1)][:], identity[:], inverse[n][:, 1:2], 0.0, ALU.mult, ALU.add
                )

        def flip_relation(i):
            a_ps[i] = []
            for first in range(0, i + 1, PER_FLIP):
                bank = flip.tile([P, PER_FLIP, P], BF16, name="a_ps", tag="flip")
                for b in range(min(PER_FLIP, i + 1 - first)):
                    history = slice((first + b) * P, (first + b + 1) * P)
                    nc.tensor.matmul(bank[:, b, :], rel_exp[i][:, history], rel_diag[i][:], start=b == 0, stop=False)
                a_ps[i].append(bank)

        def flip_scores(i):
            for g, bank in enumerate(a_ps[i]):
                first = g * PER_FLIP
                count = min(PER_FLIP, i + 1 - first)
                for b in range(count):
                    history = slice((first + b) * P, (first + b + 1) * P)
                    nc.tensor.matmul(bank[:, b, :], sc_exp[i][:, history], diag[i][:], start=False, stop=b == count - 1)

        def keep_weights(i):
            a_sb[i] = work.tile([P, BLOCKS, P], BF16, name="a_sb")
            for g, bank in enumerate(a_ps[i]):
                count = min(PER_FLIP, i + 1 - g * PER_FLIP)
                nc.vector.tensor_copy(a_sb[i][:, g * PER_FLIP : g * PER_FLIP + count, :], bank[:, :count, :])

        def mix(i):
            if i % PER_BANK == PER_BANK - 1:
                o_ps[0] = mixed.tile([P, PIECE], F32, name="o_ps")
            cols = slice((i % PER_BANK) * P, (i % PER_BANK + 1) * P)
            for j in range(i + 1):
                nc.tensor.matmul(o_ps[0][:, cols], v_sb[:, j, :], a_sb[i][:, j, :], start=j == 0, stop=j == i)
            if i < PER_BANK:
                nc.scalar.activation(
                    o_sb[:, i * P : (i + 1) * P], o_ps[0][:, cols], FUNC.Identity, bias=bv_col[:, 0:1], scale=0.5
                )
            elif i % PER_BANK == 0:
                nc.scalar.activation(
                    o_sb[:, i * P : i * P + PIECE], o_ps[0][:], FUNC.Identity, bias=bv_col[:, 0:1], scale=0.5
                )

        def project(first, m):
            cols = slice(first * P, first * P + PIECE)
            out_ps = product.tile([P, PIECE], F32, name="out_ps", tag="product")
            nc.tensor.matmul(out_ps[:], weights["out"][:, m * P : (m + 1) * P], o_sb[:, cols], start=True, stop=True)
            out_sb = store.tile([P, PIECE], F32, name="out_sb")
            nc.scalar.activation(out_sb[:], out_ps[:], FUNC.Identity, bias=b_out_cols[:, m : m + 1])
            nc.sync.dma_start(out[m * P : (m + 1) * P, cols], out_sb[:])

        def project_block(i):
            cols = slice(i * P, (i + 1) * P)
            out_ps = product.tile([P, OUT // P, P], F32, name="out_ps", tag="product")
            for m in range(OUT // P):
                nc.tensor.matmul(out_ps[:, m, :], weights["out"][:, m * P : (m + 1) * P], o_sb[:, cols], start=True, stop=True)
            out_sb = store.tile([P, OUT // P, P], F32, name="out_sb")
            nc.vector.tensor_tensor(
                out_sb[:], out_ps[:], b_out_cols[:].unsqueeze(2).to_broadcast([P, OUT // P, P]), ALU.add
            )
            nc.sync.dma_start(out.rearrange("(m p) q -> p m q", p=P)[:, :, cols], out_sb[:])

        order = list(reversed(range(BLOCKS)))

        def block(n):
            return order[n] if 0 <= n < BLOCKS else None

        make_identity(nc, identity[:])
        nc.gpsimd.memset(future[:], 0.0)
        nc.gpsimd.affine_select(
            out=future[:], in_=future[:], pattern=[[-1, P]], compare_op=ALU.is_ge,
            fill=MASKED, base=0, channel_multiplier=1,
        )
        nc.sync.dma_start(lab_row[:], lab)
        nc.sync.dma_start(table_rows[:], table.rearrange("(a p) d -> p a d", p=P))
        nc.sync.dma_start(offsets[:], offs)
        nc.scalar.dma_start(weights["right"][:], w_right)
        nc.scalar.dma_start(weights["wrong"][:], w_wrong)
        nc.scalar.dma_start(b_in_col[:], b_in)
        nc.scalar.dma_start(weights["q"][:], wq)
        nc.scalar.dma_start(bq_col[:], bq)
        for i in order:
            load_rel(i)
        nc.gpsimd.dma_start(weights["k"][:], wk)
        nc.gpsimd.dma_start(weights["v"][:], wv)
        nc.gpsimd.dma_start(bv_col[:], bv)
        nc.gpsimd.dma_start(weights["out"][:], w_out)
        with nc.allow_non_contiguous_dma(reason="one float32 to a partition and block"):
            nc.gpsimd.dma_start(b_out_cols[:], b_out.rearrange("(a p) o -> p (a o)", p=P))

        nc.vector.memset(ones[:], 1.0)
        nc.vector.memset(lab_bf16[:].bitcast(F32), 0.0)
        lab_ps = [flip.tile([P, 2, PIECE], BF16, name="lab_ps%d" % h, tag="flip") for h in range(T // PIECE // 2)]
        for piece in range(T // PIECE):
            cols = slice(piece * PIECE, (piece + 1) * PIECE)
            nc.vector.tensor_copy(lab_bf16[0:1, cols], lab_row[:, cols])
            nc.tensor.matmul(lab_ps[piece // 2][:, piece % 2, :], ones[:], lab_bf16[:, cols], start=True, stop=True)

        flipped = flip.tile([P, ITEMS], BF16, name="flipped", tag="flip")
        for a in range(ITEMS // P):
            nc.tensor.transpose(flipped[:, a * P : (a + 1) * P], table_rows[:, a, :], identity[:])
        nc.vector.tensor_copy(window[:], flipped[:])

        for piece in range(T // PIECE):
            cols = slice(piece * PIECE, (piece + 1) * PIECE)
            relu, masked = {}, {}
            for w_name in ("right", "wrong"):
                x_ps = product.tile([P, PIECE], F32, name="x_ps", tag="product")
                nc.tensor.matmul(x_ps[:], weights[w_name][:], looked_up(piece), start=True, stop=True)
                relu[w_name] = work.tile([P, PIECE], BF16, name="relu_" + w_name)
                nc.scalar.activation(relu[w_name][:], x_ps[:], FUNC.Relu, bias=b_in_col[:, 0:1])
                masked[w_name] = work.tile([P, PIECE], BF16, name="x_" + w_name)
            lab_piece = lab_ps[piece // 2][:, piece % 2, :]
            nc.vector.tensor_tensor(masked["right"][:], relu["right"][:], lab_piece, ALU.mult)
            nc.vector.scalar_tensor_tensor(
                out=masked["wrong"][:], in0=lab_piece, scalar=0.0, in1=relu["wrong"][:], op0=ALU.is_equal, op1=ALU.mult
            )
            nc.vector.tensor_tensor(x_sb[:, cols], masked["right"][:], masked["wrong"][:], ALU.max)
        for piece in range(T // PIECE):
            cols = slice(piece * PIECE, (piece + 1) * PIECE)
            q_ps = product.tile([P, PIECE], F32, name="q_ps", tag="product")
            nc.tensor.matmul(q_ps[:], weights["q"][:], looked_up(T // PIECE + piece), start=True, stop=True)
            nc.scalar.activation(q_sb[:, cols], q_ps[:], FUNC.Identity, bias=bq_col[:, 0:1])

        for piece in range(T // PIECE):
            cols = slice(piece * PIECE, (piece + 1) * PIECE)
            k_ps = product.tile([P, PIECE], F32, name="k_ps", tag="product")
            nc.tensor.matmul(k_ps[:], weights["k"][:], x_sb[:, cols], start=True, stop=True)
            nc.scalar.copy(k_sb[:, cols], k_ps[:])
        sums[-1] = work.tile([P, 2], F32, name="sums")
        relation(order[0], sums[-1][:, 1:2])
        invert(-1)
        diagonals(-1)
        for first in range(0, BLOCKS, PER_FLIP):
            v_ps = product.tile([P, PER_FLIP, P], BF16, name="v_ps", tag="product")
            for b in range(PER_FLIP):
                j = first + b
                nc.tensor.matmul(v_ps[:, b, :], x_sb[:, j * P : (j + 1) * P], weights["v"][:], start=True, stop=True)
            nc.vector.tensor_copy(v_sb[:, first : first + PER_FLIP, :], v_ps[:])

        scores(order[0])
        for n in range(BLOCKS + 2):
            now, after, before, done = block(n), block(n + 1), block(n - 1), block(n - 2)
            if now is not None:
                shift(now)
            if after is not None:
                scores(after)
            if done is not None:
                keep_weights(done)
            if now is not None:
                sums[n] = work.tile([P, 2], F32, name="sums")
                weigh(now, sums[n][:, 0:1])
            if done is not None:
                mix(done)
                m = -done % PER_BANK
                if PER_BANK <= done + m < BLOCKS:
                    project(done + m, m)
                if done < PER_BANK:
                    project_block(done)
            if before is not None:
                invert(n - 1)
            if after is not None:
                relation(after, sums[n][:, 1:2])
            if before is not None:
                diagonals(n - 1)
                flip_scores(before)
            if now is not None:
                flip_relation(now)
